import numpy as np
import ml_dtypes


def mxq(x, axis, fmt="e4m3"):
    dtype, down = {"e4m3": (ml_dtypes.float8_e4m3fn, 7), "e5m2": (ml_dtypes.float8_e5m2, 14)}[fmt]
    v = np.moveaxis(np.asarray(x, np.float32).astype(ml_dtypes.bfloat16).astype(np.float64), axis, -1)
    blocks = v.reshape(v.shape[:-1] + (-1, 32))
    amax = np.abs(blocks).max(-1, keepdims=True)
    byte = np.maximum(np.where(amax > 0, np.frexp(amax)[1] - 1 + 127, 0) - down, 1)
    scale = np.exp2(byte - 127.0)
    codes = (blocks / scale).astype(np.float32).astype(dtype).astype(np.float64)
    return np.moveaxis((codes * scale).reshape(v.shape), -1, axis)


WIDE = False


def mx_kscale(k):
    if not WIDE:
        return np.ones(k)
    levels = np.array([10, -10, 5, -5, 0])
    if k % 512:
        return np.exp2(np.random.permutation(np.resize(levels, k // 32))).repeat(32)
    a = np.empty((k // 512, 16))
    for p in range(k // 512):
        a[p, :8] = np.random.permutation(np.resize(levels, 8))
        for g in range(8):
            far = levels[np.abs(levels - a[p, g]) >= 10]
            a[p, g + 8] = far[np.random.randint(len(far))]
    return np.exp2(a.ravel()).repeat(32)


BF16 = ml_dtypes.bfloat16


def bf(x):
    return np.asarray(x, np.float32).astype(BF16)


def f64(x):
    return np.asarray(x).astype(np.float64)


B, N, SHOT, D = 2048, 1024, 5, 512
C = 2.0
GS = 4.0


def protos_of(x2):
    return f64(x2).reshape(N, SHOT, D).mean(axis=1)


def setup_inputs():
    s = mx_kscale(B)[:, None]
    u = mx_kscale(N)
    g = np.random.standard_normal(D) * C
    x1 = (g + np.random.standard_normal((B, D))) / np.sqrt(D) * s
    x2 = (g + np.random.standard_normal((N, SHOT, D)) * np.sqrt(SHOT)) / np.sqrt(D) / u[:, None, None]
    go = np.random.standard_normal((B, N)) * np.exp2(np.random.randint(-6, 1, (B, 1))) * GS / s * u[None, :]
    return {"x1": bf(x1.reshape(B, D, 1, 1)), "x2": bf(x2.reshape(N, SHOT, D, 1, 1)), "grad_out": bf(go)}


def reference(x1, x2, grad_out):
    q = f64(x1).reshape(B, D)
    p = protos_of(x2)
    g = f64(grad_out)
    r = g.sum(axis=1)[:, None]
    c = g.sum(axis=0)[:, None]
    gp = mxq(g, 1, "e5m2") @ mxq(p, 0, "e4m3")
    gq = mxq(g, 0, "e5m2").T @ mxq(q, 0, "e4m3")
    dq = 2.0 * gp - 2.0 * r * q
    dp = 2.0 * gq - 2.0 * c * p
    dx1 = dq.reshape(B, D, 1, 1)
    dx2 = np.repeat((dp / SHOT)[:, None, :], SHOT, axis=1).reshape(N, SHOT, D, 1, 1)
    return dx1, dx2

@@ -1,0 +1,335 @@
+from contextlib import ExitStack
+
+import concourse.mybir as mybir
+from concourse.masks import make_identity
+
+B, N, SHOT, D = 2048, 1024, 5, 512
+
+F32 = mybir.dt.float32
+BF16 = mybir.dt.bfloat16
+U32 = mybir.dt.uint32
+U8 = mybir.dt.uint8
+E4M3 = mybir.dt.float8_e4m3fn_x4
+E5M2 = mybir.dt.float8_e5m2_x4
+COPY = mybir.ActivationFunctionType.Copy
+ADD = mybir.AluOpType.add
+MULT = mybir.AluOpType.mult
+AXIS_X = mybir.AxisListType.X
+
+P = 128
+PASS = 512
+QP = B // PASS
+NP = N // PASS
+
+FLOPS = 2 * 2 * B * N * D
+PE_SUMS = 5
+
+
+def tile_proto_metric_v_kernel(tc, x1, x2, grad_out, out_0, out_1):
+    nc = tc.nc
+    x1_v = x1.rearrange("(g p j) d a b -> g p j (d a b)", p=P, j=4)
+    x2_v = x2.rearrange("(g p j) s d a b -> g j p s (d a b)", p=P, j=4)
+    go_v = grad_out.rearrange("(g p j) n -> g p j n", p=P, j=4)
+    o0_v = out_0.rearrange("(g p j) d a b -> g p j (d a b)", p=P, j=4)
+    o1_v = out_1.rearrange("(g p j) s d a b -> g j p s (d a b)", p=P, j=4)
+
+    with ExitStack() as ctx:
+        keep = ctx.enter_context(tc.tile_pool(name="keep", bufs=1))
+        work = ctx.enter_context(tc.tile_pool(name="work", bufs=2))
+        psum = ctx.enter_context(tc.psum_pool(name="psum", bufs=1))
+
+        wide_ident = keep.tile([P, 7 * P], F32, name="wide_ident", align_bytes=64)
+        nc.gpsimd.memset(wide_ident[:], 0.0)
+        ident = wide_ident[:, 3 * P : 4 * P]
+        make_identity(nc, ident)
+        ident_bf = keep.tile([P, P], BF16, name="ident_bf", align_bytes=64)
+        make_identity(nc, ident_bf[:])
+        ones = keep.tile([P, 2], BF16, name="ones")
+        nc.vector.memset(ones[:], 1.0)
+
+        g_raw = [keep.tile([P, 4, N], BF16, name=f"g_raw{b}", align_bytes=64) for b in range(QP)]
+        q_raw = [keep.tile([P, 4, D], BF16, name=f"q_raw{b}", align_bytes=64) for b in range(QP)]
+        g_codes = [keep.tile([P, N], U32, name=f"g_codes{b}", align_bytes=64) for b in range(QP)]
+        g_scales = [keep.tile([P, N], U8, name=f"g_scales{b}", align_bytes=64) for b in range(QP)]
+        q_codes = [keep.tile([P, D], U32, name=f"q_codes{b}", align_bytes=64) for b in range(QP)]
+        q_scales = [keep.tile([P, D], U8, name=f"q_scales{b}", align_bytes=64) for b in range(QP)]
+        t_codes = [[keep.tile([P, PASS], U32, name=f"t_codes{h}_{b}", align_bytes=64) for b in range(QP)] for h in range(NP)]
+        t_scales = [[keep.tile([P, PASS], U8, name=f"t_scales{h}_{b}", align_bytes=64) for b in range(QP)] for h in range(NP)]
+        p_codes = [keep.tile([P, D], U32, name=f"p_codes{h}", align_bytes=64) for h in range(NP)]
+        p_scales = [keep.tile([P, D], U8, name=f"p_scales{h}", align_bytes=64) for h in range(NP)]
+        sums = [keep.tile([P, 4, D], F32, name=f"sums{h}", align_bytes=64) for h in range(NP)]
+        row_m2 = keep.tile([P, 4 * QP], F32, name="row_m2")
+        c_nat = keep.tile([P, N // P], F32, name="c_nat")
+        c_neg = keep.tile([P, 4, NP], F32, name="c_neg")
+        c_parts = psum.tile([P, QP, N // P], F32, name="c_parts", tag="c")
+
+        x2_t = {}
+        gg, qg, gt, tp, acc, tmp, o0 = {}, {}, {}, {}, {}, {}, {}
+        s_ps = {}
+
+        def load_x2(n):
+            x2_t[n] = work.tile([P, SHOT, D], BF16, name="x2_t", bufs=6, align_bytes=64)
+            nc.sync.dma_start(out=x2_t[n][:], in_=x2_v[n // 4, n % 4])
+
+        def transposes(b, m):
+            h, half = m // 2, m % 2
+            if half == 0:
+                gt[b, h] = work.tile([P, PASS, 4], BF16, name="gt", bufs=5, align_bytes=64)
+            bank = psum.tile([P, 2, 2, P], F32, name="bank", tag="tp", bufs=2)
+            tp[b, m] = bank
+            for u in range(2):
+                for jj in range(2):
+                    words = g_raw[b][:, 2 * half + jj, PASS * h : PASS * (h + 1)].bitcast(F32)
+                    nc.tensor.transpose(bank[:, u, jj, :], words[:, u::2], ident)
+
+        def copy_t(b, m):
+            h, half = m // 2, m % 2
+            rows = gt[b, h][:].rearrange("p r t -> p (r t)").bitcast(F32)[:, 512 * half : 512 * (half + 1)]
+            nc.scalar.copy(
+                out=rows.rearrange("p (r u) -> p r u", u=2),
+                in_=tp[b, m][:].rearrange("p u j r -> p (j r) u"),
+            )
+
+        def quant(codes, scales, src, fmt):
+            nc.vector.quantize_mx(out=codes.bitcast(fmt), scales=scales, in_=src[:].rearrange("p c t -> p (c t)"))
+
+        def quant_t(b, h):
+            quant(t_codes[h][b][:], t_scales[h][b][:], gt[b, h], E5M2)
+
+        def group_g(b, h):
+            gg[b, h] = work.tile([P, PASS, 4], BF16, name="gg", bufs=3, align_bytes=64)
+            nc.vector.tensor_copy(
+                out=gg[b, h][:].rearrange("p (t c) j -> p t c j", t=4),
+                in_=g_raw[b][:, :, PASS * h : PASS * (h + 1)].rearrange("p j (c t) -> p t c j", t=4),
+            )
+
+        def quant_g(b, h):
+            cols = slice(PASS * h, PASS * (h + 1))
+            quant(g_codes[b][:, cols], g_scales[b][:, cols], gg[b, h], E5M2)
+
+        def group_q(b):
+            qg[b] = work.tile([P, D, 4], BF16, name="qg", bufs=2, align_bytes=64)
+            nc.scalar.copy(out=qg[b][:], in_=q_raw[b][:].rearrange("p j d -> p d j"))
+
+        def quant_q(b):
+            quant(q_codes[b][:], q_scales[b][:], qg[b], E4M3)
+
+        def col_sums(b):
+            for k in range(N // P):
+                for j in range(4):
+                    nc.tensor.matmul(
+                        c_parts[:, b, k : k + 1],
+                        lhsT=g_raw[b][:, j, P * k : P * (k + 1)],
+                        rhs=ones[:, 0:1],
+                        start=(j == 0),
+                        stop=(j == 3),
+                    )
+
+        def col_total():
+            nc.vector.tensor_reduce(out=c_nat[:], in_=c_parts[:].rearrange("p b k -> p k b"), axis=AXIS_X, op=ADD)
+
+        def col_permute():
+            c_perm = psum.tile([P, 4, NP], F32, name="c_perm", tag="c")
+            for t in range(4):
+                for kk in range(4):
+                    start = 3 * P - P * kk + t
+                    nc.tensor.matmul(
+                        c_perm[:, t, :],
+                        lhsT=wide_ident[:, start : start + 4 * P - 3 : 4],
+                        rhs=c_nat[:, kk::4],
+                        start=(kk == 0),
+                        stop=(kk == 3),
+                    )
+            nc.scalar.mul(c_neg[:], c_perm[:], -2.0 / (SHOT * SHOT))
+
+        def sum_pe(n):
+            s_ps[n] = psum.tile([P, D], F32, name="s_ps", tag="s", bufs=2)
+            for s in range(SHOT):
+                nc.tensor.matmul(s_ps[n][:], lhsT=ident_bf[:], rhs=x2_t[n][:, s, :], start=(s == 0), stop=(s == SHOT - 1))
+
+        def sum_copy(n):
+            nc.scalar.copy(out=sums[n // 4][:, n % 4, :], in_=s_ps[n][:])
+
+        def sum_v(n):
+            x = x2_t[n]
+            a = work.tile([P, D], F32, name="sum_a", bufs=1)
+            b = work.tile([P, D], F32, name="sum_b", bufs=1)
+            nc.vector.tensor_tensor(out=a[:], in0=x[:, 0, :], in1=x[:, 1, :], op=ADD)
+            nc.vector.tensor_tensor(out=b[:], in0=x[:, 2, :], in1=x[:, 3, :], op=ADD)
+            nc.vector.tensor_tensor(out=a[:], in0=a[:], in1=x[:, 4, :], op=ADD)
+            nc.vector.tensor_tensor(out=sums[n // 4][:, n % 4, :], in0=a[:], in1=b[:], op=ADD)
+
+        def scaled(n):
+            tmp[n] = work.tile([P, D], F32, name="tmp", bufs=3)
+            nc.scalar.activation(out=tmp[n][:], in_=sums[n // 4][:, n % 4, :], func=COPY, scale=c_neg[:, n % 4, n // 4 : n // 4 + 1])
+
+        pg = {}
+
+        def group_p(h):
+            pg[h] = work.tile([P, D, 4], BF16, name="pg", bufs=1, align_bytes=64)
+            nc.vector.tensor_scalar(
+                out=pg[h][:], in0=sums[h][:].rearrange("p j d -> p d j"), scalar1=2.0 / SHOT, scalar2=None, op0=MULT
+            )
+
+        def quant_p(h):
+            quant(p_codes[h][:], p_scales[h][:], pg[h], E4M3)
+
+        def mm_q(n):
+            acc["q", n] = psum.tile([P, D], F32, name="acc_q", tag="acc", bufs=3)
+            cols = slice(P * n, P * (n + 1))
+            for b in range(QP):
+                nc.tensor.matmul_mx(
+                    out=acc["q", n][:],
+                    lhsT=g_codes[b][:, cols].bitcast(E5M2),
+                    lhsT_scale=g_scales[b][:, cols],
+                    rhs=q_codes[b][:].bitcast(E4M3),
+                    rhs_scale=q_scales[b][:],
+                    start=(b == 0),
+                    stop=(b == QP - 1),
+                )
+
+        def finish_1(n):
+            o1 = work.tile([P, D], F32, name="o1", bufs=3)
+            nc.vector.scalar_tensor_tensor(out=o1[:], in0=acc["q", n][:], scalar=2.0 / SHOT, in1=tmp[n][:], op0=MULT, op1=ADD)
+            nc.sync.dma_start(out=o1_v[n // 4, n % 4], in_=o1[:].unsqueeze(1).to_broadcast([P, SHOT, D]))
+
+        def row_sum(i):
+            dump = work.tile([P, N], BF16, name="dump", bufs=2)
+            nc.scalar.activation(
+                out=dump[:], in_=g_raw[i // 4][:, i % 4, :], func=COPY, scale=-2.0, accum_out=row_m2[:, i : i + 1]
+            )
+
+        def mm_p(i):
+            b, j = i // 4, i % 4
+            acc["p", i] = psum.tile([P, D], F32, name="acc_p", tag="acc", bufs=3)
+            cols = slice(P * j, P * (j + 1))
+            for h in range(NP):
+                nc.tensor.matmul_mx(
+                    out=acc["p", i][:],
+                    lhsT=t_codes[h][b][:, cols].bitcast(E5M2),
+                    lhsT_scale=t_scales[h][b][:, cols],
+                    rhs=p_codes[h][:].bitcast(E4M3),
+                    rhs_scale=p_scales[h][:],
+                    start=(h == 0),
+                    stop=(h == NP - 1),
+                )
+
+        def finish_0(i):
+            b, j = i // 4, i % 4
+            if j % 2 == 0:
+                o0[b] = work.tile([P, 2, D], F32, name="o0", bufs=3)
+            nc.vector.scalar_tensor_tensor(
+                out=o0[b][:, j % 2, :], in0=q_raw[b][:, j, :], scalar=row_m2[:, i : i + 1], in1=acc["p", i][:], op0=MULT, op1=ADD
+            )
+            if j % 2 == 1:
+                nc.sync.dma_start(out=o0_v[b, :, j - 1 : j + 1, :], in_=o0[b][:])
+
+        with tc.manual_schedule():
+            for half in range(2):
+                nc.sync.dma_start(out=g_raw[0][:, 2 * half : 2 * half + 2, :], in_=go_v[0, :, 2 * half : 2 * half + 2, :])
+            nc.sync.dma_start(out=q_raw[0][:], in_=x1_v[0])
+            for b in range(1, QP):
+                nc.sync.dma_start(out=g_raw[b][:], in_=go_v[b])
+                nc.sync.dma_start(out=q_raw[b][:], in_=x1_v[b])
+            for n in range(6):
+                load_x2(n)
+
+            for b in range(2):
+                for m in range(4):
+                    transposes(b, m)
+                    copy_t(b, m)
+                col_sums(b)
+                group_q(b)
+                group_g(b, 0)
+                if b > 0:
+                    quant_g(b - 1, 1)
+                group_g(b, 1)
+                quant_g(b, 0)
+                if b > 0:
+                    quant_q(b - 1)
+            group_q(2)
+            group_g(2, 0)
+            quant_g(1, 1)
+            group_g(2, 1)
+            quant_g(2, 0)
+            quant_q(1)
+            col_sums(2)
+            col_sums(3)
+            group_q(3)
+            group_g(3, 0)
+            quant_g(2, 1)
+            col_total()
+            group_g(3, 1)
+            quant_g(3, 0)
+            quant_q(2)
+            sum_pe(0)
+            col_permute()
+            quant_g(3, 1)
+            sum_copy(0)
+            load_x2(6)
+            scaled(0)
+            sum_pe(1)
+            sum_copy(1)
+            load_x2(7)
+            quant_q(3)
+            for m in range(4):
+                transposes(2, m)
+                copy_t(2, m)
+            sum_pe(2)
+            quant_t(0, 0)
+            quant_t(0, 1)
+            mm_q(0)
+            scaled(1)
+            sum_copy(2)
+            sum_pe(3)
+            finish_1(0)
+            quant_t(1, 0)
+            mm_q(1)
+            quant_t(1, 1)
+            scaled(2)
+            sum_copy(3)
+            sum_pe(4)
+            sum_copy(4)
+            finish_1(1)
+            mm_q(2)
+            scaled(3)
+            group_p(0)
+            for m in range(4):
+                transposes(3, m)
+                copy_t(3, m)
+            mm_q(3)
+            sum_v(5)
+            finish_1(2)
+            quant_p(0)
+            scaled(4)
+            mm_q(4)
+            row_sum(0)
+            row_sum(1)
+            sum_v(6)
+            finish_1(3)
+            mm_q(5)
+            scaled(5)
+            row_sum(2)
+            row_sum(3)
+            sum_v(7)
+            finish_1(4)
+            scaled(6)
+            mm_q(6)
+            group_p(1)
+            quant_t(2, 0)
+            quant_p(1)
+            finish_1(5)
+            scaled(7)
+            mm_q(7)
+            for i in range(4, 8):
+                row_sum(i)
+            quant_t(2, 1)
+            quant_t(3, 0)
+            finish_1(6)
+            quant_t(3, 1)
+            finish_1(7)
+            for i in range(16):
+                mm_p(i)
+                if i + 8 < 16:
+                    row_sum(i + 8)
+                finish_0(i)

@@ -38,14 +38,24 @@ def tile_proto_metric_v_kernel(tc, x1, x2, grad_out, out_0, out_1):
         work = ctx.enter_context(tc.tile_pool(name="work", bufs=2))
         psum = ctx.enter_context(tc.psum_pool(name="psum", bufs=1))
 
-        wide_ident = keep.tile([P, 7 * P], F32, name="wide_ident", align_bytes=64)
-        nc.gpsimd.memset(wide_ident[:], 0.0)
-        ident = wide_ident[:, 3 * P : 4 * P]
-        make_identity(nc, ident)
+        ident_t = keep.tile([P, P], F32, name="ident_t", align_bytes=64)
+        make_identity(nc, ident_t[:])
+        ident = ident_t[:]
         ident_bf = keep.tile([P, P], BF16, name="ident_bf", align_bytes=64)
         make_identity(nc, ident_bf[:])
         ones = keep.tile([P, 2], BF16, name="ones")
         nc.vector.memset(ones[:], 1.0)
+        pick = keep.tile([P, 4, 4, 32], F32, name="pick", align_bytes=64)
+        nc.vector.tensor_copy(
+            out=pick[:],
+            in_=ident.rearrange("p (q t) -> p t q", t=4).unsqueeze(2).to_broadcast([P, 4, 4, 32]),
+        )
+        quarter = keep.tile([P, 4], F32, name="quarter")
+        nc.vector.tensor_reduce(out=quarter[:], in_=ident.rearrange("p (k x) -> p k x", k=4), axis=AXIS_X, op=ADD)
+        mask = keep.tile([P, 4], F32, name="mask")
+        nc.vector.tensor_scalar(
+            out=mask[:], in0=quarter[:], scalar1=-2.0 / (SHOT * SHOT), scalar2=None, op0=MULT
+        )
 
         g_raw = [keep.tile([P, 4, N], BF16, name=f"g_raw{b}", align_bytes=64) for b in range(QP)]
         q_raw = [keep.tile([P, 4, D], BF16, name=f"q_raw{b}", align_bytes=64) for b in range(QP)]
@@ -61,21 +71,21 @@ def tile_proto_metric_v_kernel(tc, x1, x2, grad_out, out_0, out_1):
         row_m2 = keep.tile([P, 4 * QP], F32, name="row_m2")
         c_nat = keep.tile([P, N // P], F32, name="c_nat")
         c_neg = keep.tile([P, 4, NP], F32, name="c_neg")
-        c_parts = psum.tile([P, QP, N // P], F32, name="c_parts", tag="c")
+        c_parts = psum.tile([P, 2 * QP, N // P], F32, name="c_parts", tag="c")
 
         x2_t = {}
         gg, qg, gt, tp, acc, tmp, o0 = {}, {}, {}, {}, {}, {}, {}
-        s_ps = {}
+        s_ps, sv = {}, {}
 
         def load_x2(n):
-            x2_t[n] = work.tile([P, SHOT, D], BF16, name="x2_t", bufs=6, align_bytes=64)
+            x2_t[n] = work.tile([P, SHOT, D], BF16, name="x2_t", tag="big", bufs=8, align_bytes=64)
             nc.sync.dma_start(out=x2_t[n][:], in_=x2_v[n // 4, n % 4])
 
         def transposes(b, m):
             h, half = m // 2, m % 2
             if half == 0:
-                gt[b, h] = work.tile([P, PASS, 4], BF16, name="gt", bufs=5, align_bytes=64)
-            bank = psum.tile([P, 2, 2, P], F32, name="bank", tag="tp", bufs=2)
+                gt[b, h] = work.tile([P, PASS, 4], BF16, name="gt", bufs=4, align_bytes=64)
+            bank = psum.tile([P, 2, 2, P], F32, name="bank", tag="x", bufs=4)
             tp[b, m] = bank
             for u in range(2):
                 for jj in range(2):
@@ -99,8 +109,8 @@ def tile_proto_metric_v_kernel(tc, x1, x2, grad_out, out_0, out_1):
         def group_g(b, h):
             gg[b, h] = work.tile([P, PASS, 4], BF16, name="gg", bufs=3, align_bytes=64)
             nc.vector.tensor_copy(
-                out=gg[b, h][:].rearrange("p (t c) j -> p t c j", t=4),
-                in_=g_raw[b][:, :, PASS * h : PASS * (h + 1)].rearrange("p j (c t) -> p t c j", t=4),
+                out=gg[b, h][:].rearrange("p (t c) j -> p c t j", t=4),
+                in_=g_raw[b][:, :, PASS * h : PASS * (h + 1)].rearrange("p j (c t) -> p c t j", t=4),
             )
 
         def quant_g(b, h):
@@ -115,49 +125,67 @@ def tile_proto_metric_v_kernel(tc, x1, x2, grad_out, out_0, out_1):
             quant(q_codes[b][:], q_scales[b][:], qg[b], E4M3)
 
         def col_sums(b):
-            for k in range(N // P):
-                for j in range(4):
-                    nc.tensor.matmul(
-                        c_parts[:, b, k : k + 1],
-                        lhsT=g_raw[b][:, j, P * k : P * (k + 1)],
-                        rhs=ones[:, 0:1],
-                        start=(j == 0),
-                        stop=(j == 3),
-                    )
+            for half in range(2):
+                for k in range(N // P):
+                    for j in range(2):
+                        nc.tensor.matmul(
+                            c_parts[:, 2 * b + half, k : k + 1],
+                            lhsT=g_raw[b][:, 2 * half + j, P * k : P * (k + 1)],
+                            rhs=ones[:, 0:1],
+                            start=(j == 0),
+                            stop=(j == 1),
+                        )
 
         def col_total():
             nc.vector.tensor_reduce(out=c_nat[:], in_=c_parts[:].rearrange("p b k -> p k b"), axis=AXIS_X, op=ADD)
 
+        c_all = {}
+
         def col_permute():
-            c_perm = psum.tile([P, 4, NP], F32, name="c_perm", tag="c")
+            c_all[0] = psum.tile([P, 4, NP * 4], F32, name="c_perm", tag="c")
             for t in range(4):
-                for kk in range(4):
-                    start = 3 * P - P * kk + t
-                    nc.tensor.matmul(
-                        c_perm[:, t, :],
-                        lhsT=wide_ident[:, start : start + 4 * P - 3 : 4],
-                        rhs=c_nat[:, kk::4],
-                        start=(kk == 0),
-                        stop=(kk == 3),
-                    )
-            nc.scalar.mul(c_neg[:], c_perm[:], -2.0 / (SHOT * SHOT))
+                nc.tensor.matmul(
+                    c_all[0][:, t, :],
+                    lhsT=pick[:, t, :, :].rearrange("p r q -> p (r q)"),
+                    rhs=c_nat[:],
+                    start=True,
+                    stop=True,
+                )
+
+        c_prod = keep.tile([P, 4 * NP, 4], F32, name="c_prod")
+
+        def col_mask():
+            nc.vector.tensor_tensor(
+                out=c_prod[:],
+                in0=c_all[0][:].rearrange("p t (h k) -> p (t h) k", k=4),
+                in1=mask[:].unsqueeze(1).to_broadcast([P, 4 * NP, 4]),
+                op=MULT,
+            )
+
+        def col_pick():
+            nc.vector.tensor_reduce(out=c_neg[:].rearrange("p t h -> p (t h)"), in_=c_prod[:], axis=AXIS_X, op=ADD)
 
         def sum_pe(n):
-            s_ps[n] = psum.tile([P, D], F32, name="s_ps", tag="s", bufs=2)
+            s_ps[n] = psum.tile([P, D], F32, name="s_ps", tag="x", bufs=4)
             for s in range(SHOT):
                 nc.tensor.matmul(s_ps[n][:], lhsT=ident_bf[:], rhs=x2_t[n][:, s, :], start=(s == 0), stop=(s == SHOT - 1))
 
         def sum_copy(n):
             nc.scalar.copy(out=sums[n // 4][:, n % 4, :], in_=s_ps[n][:])
 
-        def sum_v(n):
+        def sum_v(n, part):
             x = x2_t[n]
-            a = work.tile([P, D], F32, name="sum_a", bufs=1)
-            b = work.tile([P, D], F32, name="sum_b", bufs=1)
-            nc.vector.tensor_tensor(out=a[:], in0=x[:, 0, :], in1=x[:, 1, :], op=ADD)
-            nc.vector.tensor_tensor(out=b[:], in0=x[:, 2, :], in1=x[:, 3, :], op=ADD)
-            nc.vector.tensor_tensor(out=a[:], in0=a[:], in1=x[:, 4, :], op=ADD)
-            nc.vector.tensor_tensor(out=sums[n // 4][:, n % 4, :], in0=a[:], in1=b[:], op=ADD)
+            if part == 0:
+                sv[n] = (work.tile([P, D], F32, name="sum_a", bufs=1), work.tile([P, D], F32, name="sum_b", bufs=1))
+            a, b = sv[n]
+            if part == 0:
+                nc.vector.tensor_tensor(out=a[:], in0=x[:, 0, :], in1=x[:, 1, :], op=ADD)
+            if part == 1:
+                nc.vector.tensor_tensor(out=b[:], in0=x[:, 2, :], in1=x[:, 3, :], op=ADD)
+            if part == 2:
+                nc.vector.tensor_tensor(out=a[:], in0=a[:], in1=x[:, 4, :], op=ADD)
+            if part == 3:
+                nc.vector.tensor_tensor(out=sums[n // 4][:, n % 4, :], in0=a[:], in1=b[:], op=ADD)
 
         def scaled(n):
             tmp[n] = work.tile([P, D], F32, name="tmp", bufs=3)
@@ -189,7 +217,7 @@ def tile_proto_metric_v_kernel(tc, x1, x2, grad_out, out_0, out_1):
                 )
 
         def finish_1(n):
-            o1 = work.tile([P, D], F32, name="o1", bufs=3)
+            o1 = work.tile([P, D], F32, name="o1", tag="big", bufs=8, align_bytes=64)
             nc.vector.scalar_tensor_tensor(out=o1[:], in0=acc["q", n][:], scalar=2.0 / SHOT, in1=tmp[n][:], op0=MULT, op1=ADD)
             nc.sync.dma_start(out=o1_v[n // 4, n % 4], in_=o1[:].unsqueeze(1).to_broadcast([P, SHOT, D]))
 
@@ -217,7 +245,7 @@ def tile_proto_metric_v_kernel(tc, x1, x2, grad_out, out_0, out_1):
         def finish_0(i):
             b, j = i // 4, i % 4
             if j % 2 == 0:
-                o0[b] = work.tile([P, 2, D], F32, name="o0", bufs=3)
+                o0[b] = work.tile([P, 2, D], F32, name="o0", tag="big", bufs=8, align_bytes=64)
             nc.vector.scalar_tensor_tensor(
                 out=o0[b][:, j % 2, :], in0=q_raw[b][:, j, :], scalar=row_m2[:, i : i + 1], in1=acc["p", i][:], op0=MULT, op1=ADD
             )
@@ -231,105 +259,129 @@ def tile_proto_metric_v_kernel(tc, x1, x2, grad_out, out_0, out_1):
             for b in range(1, QP):
                 nc.sync.dma_start(out=g_raw[b][:], in_=go_v[b])
                 nc.sync.dma_start(out=q_raw[b][:], in_=x1_v[b])
-            for n in range(6):
+            for n in range(8):
                 load_x2(n)
 
-            for b in range(2):
-                for m in range(4):
+            def T(*banks):
+                for b, m in banks:
                     transposes(b, m)
+                for b, m in banks:
                     copy_t(b, m)
-                col_sums(b)
-                group_q(b)
-                group_g(b, 0)
-                if b > 0:
-                    quant_g(b - 1, 1)
-                group_g(b, 1)
-                quant_g(b, 0)
-                if b > 0:
-                    quant_q(b - 1)
-            group_q(2)
-            group_g(2, 0)
-            quant_g(1, 1)
-            group_g(2, 1)
-            quant_g(2, 0)
-            quant_q(1)
-            col_sums(2)
-            col_sums(3)
-            group_q(3)
-            group_g(3, 0)
-            quant_g(2, 1)
-            col_total()
-            group_g(3, 1)
-            quant_g(3, 0)
-            quant_q(2)
-            sum_pe(0)
-            col_permute()
-            quant_g(3, 1)
-            sum_copy(0)
-            load_x2(6)
-            scaled(0)
-            sum_pe(1)
-            sum_copy(1)
-            load_x2(7)
-            quant_q(3)
-            for m in range(4):
-                transposes(2, m)
-                copy_t(2, m)
-            sum_pe(2)
-            quant_t(0, 0)
-            quant_t(0, 1)
-            mm_q(0)
-            scaled(1)
-            sum_copy(2)
-            sum_pe(3)
-            finish_1(0)
-            quant_t(1, 0)
-            mm_q(1)
-            quant_t(1, 1)
-            scaled(2)
-            sum_copy(3)
-            sum_pe(4)
-            sum_copy(4)
-            finish_1(1)
-            mm_q(2)
-            scaled(3)
-            group_p(0)
-            for m in range(4):
-                transposes(3, m)
-                copy_t(3, m)
-            mm_q(3)
-            sum_v(5)
-            finish_1(2)
-            quant_p(0)
-            scaled(4)
-            mm_q(4)
+
             row_sum(0)
             row_sum(1)
-            sum_v(6)
-            finish_1(3)
-            mm_q(5)
-            scaled(5)
+            col_sums(0)
+            group_g(0, 0)
+            group_q(0)
+            group_g(0, 1)
+            quant_g(0, 0)
             row_sum(2)
             row_sum(3)
-            sum_v(7)
+            col_sums(1)
+            group_g(1, 0)
+            quant_g(0, 1)
+            quant_q(0)
+            group_q(1)
+            group_g(1, 1)
+            quant_g(1, 0)
+            col_sums(2)
+            group_g(2, 0)
+            quant_g(1, 1)
+            quant_q(1)
+            row_sum(4)
+            group_q(2)
+            group_g(2, 1)
+            quant_g(2, 0)
+            col_sums(3)
+            group_g(3, 0)
+            quant_g(2, 1)
+            quant_q(2)
+            group_q(3)
+            group_g(3, 1)
+            quant_g(3, 0)
+            row_sum(5)
+            row_sum(6)
+            sum_pe(0)
+            sum_copy(0)
+            quant_g(3, 1)
+            col_total()
+            col_permute()
+            sum_pe(1)
+            row_sum(7)
+            sum_copy(1)
+            quant_q(3)
+            sum_v(3, 0)
+            col_mask()
+            sum_v(3, 1)
+            col_pick()
+            sum_v(3, 2)
+            mm_q(0)
+            scaled(0)
+            scaled(1)
+            finish_1(0)
+            sum_v(3, 3)
+            mm_q(1)
+            sum_pe(2)
+            row_sum(8)
+            sum_copy(2)
+            scaled(2)
+            finish_1(1)
+            scaled(3)
+            mm_q(2)
+            sum_v(5, 0)
+            sum_v(5, 1)
+            sum_pe(4)
+            sum_copy(4)
+            finish_1(2)
+            mm_q(3)
+            sum_v(5, 2)
+            finish_1(3)
+            sum_v(5, 3)
+            scaled(4)
+            scaled(5)
+            mm_q(4)
+            T((0, 0), (0, 1))
+            group_p(0)
+            sum_v(7, 0)
             finish_1(4)
+            mm_q(5)
+            sum_pe(6)
+            row_sum(9)
+            sum_copy(6)
             scaled(6)
-            mm_q(6)
-            group_p(1)
-            quant_t(2, 0)
-            quant_p(1)
+            sum_v(7, 1)
             finish_1(5)
+            quant_p(0)
+            T((0, 2), (0, 3), (1, 0))
+            sum_v(7, 2)
+            quant_t(0, 0)
+            sum_v(7, 3)
             scaled(7)
-            mm_q(7)
-            for i in range(4, 8):
-                row_sum(i)
-            quant_t(2, 1)
-            quant_t(3, 0)
+            mm_q(6)
             finish_1(6)
-            quant_t(3, 1)
+            group_p(1)
+            mm_q(7)
+            T((1, 1), (1, 2), (1, 3))
+            quant_t(0, 1)
+            quant_p(1)
             finish_1(7)
+            quant_t(1, 0)
+            T((2, 0), (2, 1))
+            quant_t(1, 1)
             for i in range(16):
+                if i == 2:
+                    T((2, 2), (2, 3), (3, 0))
+                if i == 3:
+                    quant_t(2, 0)
+                if i == 4:
+                    quant_t(2, 1)
+                if i == 5:
+                    T((3, 1), (3, 2), (3, 3))
+                if i == 7:
+                    quant_t(3, 0)
+                if i == 9:
+                    quant_t(3, 1)
                 mm_p(i)
-                if i + 8 < 16:
-                    row_sum(i + 8)
+                if i + 10 < 16:
+                    row_sum(i + 10)
                 finish_0(i)

@@ -84,7 +84,7 @@ def tile_proto_metric_v_kernel(tc, x1, x2, grad_out, out_0, out_1):
         def transposes(b, m):
             h, half = m // 2, m % 2
             if half == 0:
-                gt[b, h] = work.tile([P, PASS, 4], BF16, name="gt", bufs=4, align_bytes=64)
+                gt[b, h] = work.tile([P, PASS, 4], BF16, name="gt", bufs=6, align_bytes=64)
             bank = psum.tile([P, 2, 2, P], F32, name="bank", tag="x", bufs=4)
             tp[b, m] = bank
             for u in range(2):
@@ -106,11 +106,11 @@ def tile_proto_metric_v_kernel(tc, x1, x2, grad_out, out_0, out_1):
         def quant_t(b, h):
             quant(t_codes[h][b][:], t_scales[h][b][:], gt[b, h], E5M2)
 
-        def group_g(b, h):
+        def group_g(b, h, copy=nc.vector.tensor_copy):
             gg[b, h] = work.tile([P, PASS, 4], BF16, name="gg", bufs=3, align_bytes=64)
-            nc.vector.tensor_copy(
-                out=gg[b, h][:].rearrange("p (t c) j -> p c t j", t=4),
-                in_=g_raw[b][:, :, PASS * h : PASS * (h + 1)].rearrange("p j (c t) -> p c t j", t=4),
+            copy(
+                out=gg[b, h][:].rearrange("p (t c) j -> p c j t", t=4),
+                in_=g_raw[b][:, :, PASS * h : PASS * (h + 1)].rearrange("p j (c t) -> p c j t", t=4),
             )
 
         def quant_g(b, h):
@@ -119,7 +119,10 @@ def tile_proto_metric_v_kernel(tc, x1, x2, grad_out, out_0, out_1):
 
         def group_q(b):
             qg[b] = work.tile([P, D, 4], BF16, name="qg", bufs=2, align_bytes=64)
-            nc.scalar.copy(out=qg[b][:], in_=q_raw[b][:].rearrange("p j d -> p d j"))
+            nc.scalar.copy(
+                out=qg[b][:].rearrange("p (d i) j -> p d j i", i=4),
+                in_=q_raw[b][:].rearrange("p j (d i) -> p d j i", i=4),
+            )
 
         def quant_q(b):
             quant(q_codes[b][:], q_scales[b][:], qg[b], E4M3)
@@ -189,7 +192,9 @@ def tile_proto_metric_v_kernel(tc, x1, x2, grad_out, out_0, out_1):
 
         def scaled(n):
             tmp[n] = work.tile([P, D], F32, name="tmp", bufs=3)
-            nc.scalar.activation(out=tmp[n][:], in_=sums[n // 4][:, n % 4, :], func=COPY, scale=c_neg[:, n % 4, n // 4 : n // 4 + 1])
+            nc.vector.tensor_scalar(
+                out=tmp[n][:], in0=sums[n // 4][:, n % 4, :], scalar1=c_neg[:, n % 4, n // 4 : n // 4 + 1], scalar2=None, op0=MULT
+            )
 
         pg = {}
 
@@ -216,10 +221,25 @@ def tile_proto_metric_v_kernel(tc, x1, x2, grad_out, out_0, out_1):
                     stop=(b == QP - 1),
                 )
 
+        o1 = {}
+
         def finish_1(n):
-            o1 = work.tile([P, D], F32, name="o1", tag="big", bufs=8, align_bytes=64)
-            nc.vector.scalar_tensor_tensor(out=o1[:], in0=acc["q", n][:], scalar=2.0 / SHOT, in1=tmp[n][:], op0=MULT, op1=ADD)
-            nc.sync.dma_start(out=o1_v[n // 4, n % 4], in_=o1[:].unsqueeze(1).to_broadcast([P, SHOT, D]))
+            o1[n] = work.tile([P, 2, D], F32, name="o1", tag="big", bufs=8, align_bytes=64)
+            nc.vector.scalar_tensor_tensor(
+                out=o1[n][:, 0, :], in0=acc["q", n][:], scalar=2.0 / SHOT, in1=tmp[n][:], op0=MULT, op1=ADD
+            )
+
+        def send_1(n, double=True):
+            dst = o1_v[n // 4, n % 4]
+            if not double:
+                nc.sync.dma_start(out=dst, in_=o1[n][:, 0, :].unsqueeze(1).to_broadcast([P, SHOT, D]))
+                return
+            nc.vector.tensor_copy(out=o1[n][:, 1, :], in_=o1[n][:, 0, :])
+            nc.sync.dma_start(
+                out=dst[:, 0:4, :].rearrange("p (r s) d -> p r (s d)", s=2),
+                in_=o1[n][:].rearrange("p s d -> p (s d)").unsqueeze(1).to_broadcast([P, 2, 2 * D]),
+            )
+            nc.sync.dma_start(out=dst[:, 4, :], in_=o1[n][:, 0, :])
 
         def row_sum(i):
             dump = work.tile([P, N], BF16, name="dump", bufs=2)
@@ -275,113 +295,120 @@ def tile_proto_metric_v_kernel(tc, x1, x2, grad_out, out_0, out_1):
             group_q(0)
             group_g(0, 1)
             quant_g(0, 0)
-            row_sum(2)
-            row_sum(3)
             col_sums(1)
             group_g(1, 0)
             quant_g(0, 1)
+            group_g(1, 1, nc.scalar.copy)
             quant_q(0)
             group_q(1)
-            group_g(1, 1)
             quant_g(1, 0)
+            quant_g(1, 1)
             col_sums(2)
             group_g(2, 0)
-            quant_g(1, 1)
+            group_g(2, 1, nc.scalar.copy)
             quant_q(1)
-            row_sum(4)
-            group_q(2)
-            group_g(2, 1)
             quant_g(2, 0)
+            group_q(2)
             col_sums(3)
             group_g(3, 0)
             quant_g(2, 1)
-            quant_q(2)
             group_q(3)
             group_g(3, 1)
+            quant_q(2)
             quant_g(3, 0)
-            row_sum(5)
-            row_sum(6)
             sum_pe(0)
+            row_sum(2)
             sum_copy(0)
             quant_g(3, 1)
             col_total()
             col_permute()
-            sum_pe(1)
-            row_sum(7)
-            sum_copy(1)
             quant_q(3)
-            sum_v(3, 0)
-            col_mask()
-            sum_v(3, 1)
-            col_pick()
-            sum_v(3, 2)
             mm_q(0)
+            row_sum(3)
+            sum_v(2, 0)
+            sum_v(2, 1)
+            col_mask()
+            sum_v(2, 2)
+            col_pick()
+            sum_pe(1)
+            sum_copy(1)
+            sum_v(2, 3)
             scaled(0)
-            scaled(1)
-            finish_1(0)
-            sum_v(3, 3)
             mm_q(1)
-            sum_pe(2)
-            row_sum(8)
-            sum_copy(2)
+            finish_1(0)
+            send_1(0, double=False)
+            scaled(1)
+            sum_pe(3)
+            row_sum(4)
+            sum_copy(3)
+            mm_q(2)
             scaled(2)
             finish_1(1)
-            scaled(3)
-            mm_q(2)
             sum_v(5, 0)
-            sum_v(5, 1)
-            sum_pe(4)
-            sum_copy(4)
-            finish_1(2)
+            send_1(1)
+            T((0, 0), (0, 1))
             mm_q(3)
+            finish_1(2)
+            scaled(3)
+            send_1(2)
+            sum_v(5, 1)
             sum_v(5, 2)
+            sum_pe(4)
             finish_1(3)
+            row_sum(5)
+            sum_copy(4)
             sum_v(5, 3)
+            send_1(3)
+            mm_q(4)
+            T((0, 2), (0, 3))
+            group_p(0)
             scaled(4)
             scaled(5)
-            mm_q(4)
-            T((0, 0), (0, 1))
-            group_p(0)
-            sum_v(7, 0)
             finish_1(4)
             mm_q(5)
+            sum_v(7, 0)
+            send_1(4)
+            T((1, 0), (1, 1))
             sum_pe(6)
-            row_sum(9)
-            sum_copy(6)
-            scaled(6)
-            sum_v(7, 1)
             finish_1(5)
+            sum_copy(6)
+            sum_v(7, 1)
+            send_1(5)
             quant_p(0)
-            T((0, 2), (0, 3), (1, 0))
+            T((1, 2), (1, 3))
             sum_v(7, 2)
             quant_t(0, 0)
+            scaled(6)
             sum_v(7, 3)
-            scaled(7)
             mm_q(6)
-            finish_1(6)
-            group_p(1)
-            mm_q(7)
-            T((1, 1), (1, 2), (1, 3))
             quant_t(0, 1)
-            quant_p(1)
+            finish_1(6)
+            scaled(7)
+            send_1(6)
+            mm_q(7)
+            T((2, 0), (2, 1))
+            group_p(1)
+            row_sum(6)
             finish_1(7)
             quant_t(1, 0)
-            T((2, 0), (2, 1))
+            send_1(7)
+            T((2, 2), (2, 3))
+            quant_p(1)
+            row_sum(7)
             quant_t(1, 1)
             for i in range(16):
                 if i == 2:
-                    T((2, 2), (2, 3), (3, 0))
-                if i == 3:
-                    quant_t(2, 0)
+                    T((3, 0), (3, 1))
                 if i == 4:
-                    quant_t(2, 1)
+                    quant_t(2, 0)
+                    T((3, 2), (3, 3))
                 if i == 5:
-                    T((3, 1), (3, 2), (3, 3))
-                if i == 7:
+                    quant_t(2, 1)
+                if i == 8:
                     quant_t(3, 0)
-                if i == 9:
+                if i == 10:
                     quant_t(3, 1)
                 mm_p(i)
-                if i + 10 < 16:
-                    row_sum(i + 10)
+                if i + 8 < 16:
+                    row_sum(i + 8)
                 finish_0(i)

@@ -28,10 +28,10 @@ PE_SUMS = 5
 def tile_proto_metric_v_kernel(tc, x1, x2, grad_out, out_0, out_1):
     nc = tc.nc
     x1_v = x1.rearrange("(g p j) d a b -> g p j (d a b)", p=P, j=4)
-    x2_v = x2.rearrange("(g p j) s d a b -> g j p s (d a b)", p=P, j=4)
+    x2_v = x2.rearrange("(g p h e) s d a b -> g h p e s (d a b)", p=P, h=2, e=2)
     go_v = grad_out.rearrange("(g p j) n -> g p j n", p=P, j=4)
     o0_v = out_0.rearrange("(g p j) d a b -> g p j (d a b)", p=P, j=4)
-    o1_v = out_1.rearrange("(g p j) s d a b -> g j p s (d a b)", p=P, j=4)
+    o1_v = out_1.rearrange("(g p h e) s d a b -> g h p (e s) (d a b)", p=P, h=2, e=2)
 
     with ExitStack() as ctx:
         keep = ctx.enter_context(tc.tile_pool(name="keep", bufs=1))
@@ -77,9 +77,11 @@ def tile_proto_metric_v_kernel(tc, x1, x2, grad_out, out_0, out_1):
         gg, qg, gt, tp, acc, tmp, o0 = {}, {}, {}, {}, {}, {}, {}
         s_ps, sv = {}, {}
 
-        def load_x2(n):
-            x2_t[n] = work.tile([P, SHOT, D], BF16, name="x2_t", tag="big", bufs=8, align_bytes=64)
-            nc.sync.dma_start(out=x2_t[n][:], in_=x2_v[n // 4, n % 4])
+        def load_x2(pair):
+            tile = work.tile([P, 2, SHOT, D], BF16, name="x2_pair", tag="big", bufs=4, align_bytes=64)
+            nc.sync.dma_start(out=tile[:], in_=x2_v[pair // 2, pair % 2])
+            for e in range(2):
+                x2_t[2 * pair + e] = tile[:, e, :, :]
 
         def transposes(b, m):
             h, half = m // 2, m % 2
@@ -198,11 +200,9 @@ def tile_proto_metric_v_kernel(tc, x1, x2, grad_out, out_0, out_1):
 
         pg = {}
 
-        def group_p(h):
+        def group_p(h, scale=nc.vector.tensor_scalar_mul):
             pg[h] = work.tile([P, D, 4], BF16, name="pg", bufs=1, align_bytes=64)
-            nc.vector.tensor_scalar(
-                out=pg[h][:], in0=sums[h][:].rearrange("p j d -> p d j"), scalar1=2.0 / SHOT, scalar2=None, op0=MULT
-            )
+            scale(pg[h][:], sums[h][:].rearrange("p j d -> p d j"), 2.0 / SHOT)
 
         def quant_p(h):
             quant(p_codes[h][:], p_scales[h][:], pg[h], E4M3)
@@ -224,22 +224,25 @@ def tile_proto_metric_v_kernel(tc, x1, x2, grad_out, out_0, out_1):
         o1 = {}
 
         def finish_1(n):
-            o1[n] = work.tile([P, 2, D], F32, name="o1", tag="big", bufs=8, align_bytes=64)
+            pair, e = n // 2, n % 2
+            if e == 0:
+                o1[pair] = work.tile([P, 4, D], F32, name="o1", tag="big", bufs=4, align_bytes=64)
             nc.vector.scalar_tensor_tensor(
-                out=o1[n][:, 0, :], in0=acc["q", n][:], scalar=2.0 / SHOT, in1=tmp[n][:], op0=MULT, op1=ADD
+                out=o1[pair][:, 2 * e, :], in0=acc["q", n][:], scalar=2.0 / SHOT, in1=tmp[n][:], op0=MULT, op1=ADD
             )
 
-        def send_1(n, double=True):
-            dst = o1_v[n // 4, n % 4]
-            if not double:
-                nc.sync.dma_start(out=dst, in_=o1[n][:, 0, :].unsqueeze(1).to_broadcast([P, SHOT, D]))
-                return
-            nc.vector.tensor_copy(out=o1[n][:, 1, :], in_=o1[n][:, 0, :])
+        def send_1(n):
+            pair, e = n // 2, n % 2
+            dst = o1_v[pair // 2, pair % 2]
+            src = o1[pair]
+            nc.vector.tensor_copy(out=src[:, 2 * e + 1, :], in_=src[:, 2 * e, :])
+            if e == 1:
+                nc.sync.dma_start(out=dst[:, 4:6, :], in_=src[:, 1:3, :])
+            rows = dst[:, 6 * e : 6 * e + 4, :].rearrange("p (r s) d -> p r (s d)", s=2)
             nc.sync.dma_start(
-                out=dst[:, 0:4, :].rearrange("p (r s) d -> p r (s d)", s=2),
-                in_=o1[n][:].rearrange("p s d -> p (s d)").unsqueeze(1).to_broadcast([P, 2, 2 * D]),
+                out=rows,
+                in_=src[:, 2 * e : 2 * e + 2, :].rearrange("p s d -> p (s d)").unsqueeze(1).to_broadcast([P, 2, 2 * D]),
             )
-            nc.sync.dma_start(out=dst[:, 4, :], in_=o1[n][:, 0, :])
 
         def row_sum(i):
             dump = work.tile([P, N], BF16, name="dump", bufs=2)
@@ -264,13 +267,14 @@ def tile_proto_metric_v_kernel(tc, x1, x2, grad_out, out_0, out_1):
 
         def finish_0(i):
             b, j = i // 4, i % 4
-            if j % 2 == 0:
-                o0[b] = work.tile([P, 2, D], F32, name="o0", tag="big", bufs=8, align_bytes=64)
+            if j == 0:
+                o0[b] = work.tile([P, 4, D], F32, name="o0", tag="big", bufs=4, align_bytes=64)
             nc.vector.scalar_tensor_tensor(
-                out=o0[b][:, j % 2, :], in0=q_raw[b][:, j, :], scalar=row_m2[:, i : i + 1], in1=acc["p", i][:], op0=MULT, op1=ADD
+                out=o0[b][:, j, :], in0=q_raw[b][:, j, :], scalar=row_m2[:, i : i + 1], in1=acc["p", i][:], op0=MULT, op1=ADD
             )
-            if j % 2 == 1:
-                nc.sync.dma_start(out=o0_v[b, :, j - 1 : j + 1, :], in_=o0[b][:])
+            cut = {3: 0} if b == 0 else {1: 0, 3: 2}
+            if j in cut:
+                nc.sync.dma_start(out=o0_v[b, :, cut[j] : j + 1, :], in_=o0[b][:, cut[j] : j + 1, :])
 
         with tc.manual_schedule():
             for half in range(2):
@@ -279,8 +283,8 @@ def tile_proto_metric_v_kernel(tc, x1, x2, grad_out, out_0, out_1):
             for b in range(1, QP):
                 nc.sync.dma_start(out=g_raw[b][:], in_=go_v[b])
                 nc.sync.dma_start(out=q_raw[b][:], in_=x1_v[b])
-            for n in range(8):
-                load_x2(n)
+            for pair in range(4):
+                load_x2(pair)
 
             def T(*banks):
                 for b, m in banks:
@@ -295,6 +299,8 @@ def tile_proto_metric_v_kernel(tc, x1, x2, grad_out, out_0, out_1):
             group_q(0)
             group_g(0, 1)
             quant_g(0, 0)
+            transposes(0, 0)
+            transposes(0, 1)
             col_sums(1)
             group_g(1, 0)
             quant_g(0, 1)
@@ -317,7 +323,8 @@ def tile_proto_metric_v_kernel(tc, x1, x2, grad_out, out_0, out_1):
             quant_q(2)
             quant_g(3, 0)
             sum_pe(0)
-            row_sum(2)
+            copy_t(0, 0)
+            copy_t(0, 1)
             sum_copy(0)
             quant_g(3, 1)
             col_total()
@@ -325,28 +332,30 @@ def tile_proto_metric_v_kernel(tc, x1, x2, grad_out, out_0, out_1):
             quant_q(3)
             mm_q(0)
             row_sum(3)
-            sum_v(2, 0)
-            sum_v(2, 1)
+            sum_v(1, 0)
             col_mask()
-            sum_v(2, 2)
+            sum_v(1, 1)
             col_pick()
-            sum_pe(1)
-            sum_copy(1)
-            sum_v(2, 3)
+            sum_v(1, 2)
             scaled(0)
-            mm_q(1)
+            sum_v(1, 3)
+            sum_pe(2)
+            sum_copy(2)
             finish_1(0)
-            send_1(0, double=False)
+            mm_q(1)
             scaled(1)
+            send_1(0)
             sum_pe(3)
             row_sum(4)
             sum_copy(3)
+            finish_1(1)
             mm_q(2)
             scaled(2)
-            finish_1(1)
             sum_v(5, 0)
             send_1(1)
-            T((0, 0), (0, 1))
+            row_sum(2)
+            row_sum(5)
+            T((0, 2), (0, 3))
             mm_q(3)
             finish_1(2)
             scaled(3)
@@ -355,12 +364,13 @@ def tile_proto_metric_v_kernel(tc, x1, x2, grad_out, out_0, out_1):
             sum_v(5, 2)
             sum_pe(4)
             finish_1(3)
-            row_sum(5)
+            row_sum(6)
             sum_copy(4)
             sum_v(5, 3)
             send_1(3)
             mm_q(4)
-            T((0, 2), (0, 3))
+            row_sum(7)
+            T((1, 0), (1, 1))
             group_p(0)
             scaled(4)
             scaled(5)
@@ -368,14 +378,16 @@ def tile_proto_metric_v_kernel(tc, x1, x2, grad_out, out_0, out_1):
             mm_q(5)
             sum_v(7, 0)
             send_1(4)
-            T((1, 0), (1, 1))
+            row_sum(8)
+            T((1, 2), (1, 3))
             sum_pe(6)
             finish_1(5)
+            row_sum(9)
             sum_copy(6)
             sum_v(7, 1)
             send_1(5)
             quant_p(0)
-            T((1, 2), (1, 3))
+            T((2, 0), (2, 1))
             sum_v(7, 2)
             quant_t(0, 0)
             scaled(6)
@@ -386,22 +398,21 @@ def tile_proto_metric_v_kernel(tc, x1, x2, grad_out, out_0, out_1):
             scaled(7)
             send_1(6)
             mm_q(7)
-            T((2, 0), (2, 1))
-            group_p(1)
-            row_sum(6)
+            row_sum(10)
+            group_p(1, nc.scalar.mul)
+            T((2, 2), (2, 3))
             finish_1(7)
             quant_t(1, 0)
             send_1(7)
-            T((2, 2), (2, 3))
-            quant_p(1)
-            row_sum(7)
             quant_t(1, 1)
+            quant_p(1)
             for i in range(16):
                 if i == 2:
                     T((3, 0), (3, 1))
-                if i == 4:
-                    quant_t(2, 0)
+                if i == 5:
                     T((3, 2), (3, 3))
+                if i == 3:
+                    quant_t(2, 0)
                 if i == 5:
                     quant_t(2, 1)
                 if i == 8:
@@ -409,6 +420,6 @@ def tile_proto_metric_v_kernel(tc, x1, x2, grad_out, out_0, out_1):
                 if i == 10:
                     quant_t(3, 1)
                 mm_p(i)
-                if i + 8 < 16:
+                if 3 <= i < 8:
                     row_sum(i + 8)
                 finish_0(i)

@@ -4,6 +4,7 @@ import concourse.mybir as mybir
 from concourse.masks import make_identity
 
 B, N, SHOT, D = 2048, 1024, 5, 512
+FLOPS = 2 * 2 * B * N * D
 
 F32 = mybir.dt.float32
 BF16 = mybir.dt.bfloat16
@@ -17,409 +18,456 @@ MULT = mybir.AluOpType.mult
 AXIS_X = mybir.AxisListType.X
 
 P = 128
-PASS = 512
-QP = B // PASS
-NP = N // PASS
+SLOT = 4
+PASS = P * SLOT
+B_PASSES = B // PASS
+N_PASSES = N // PASS
+N_BLOCKS = N // P
 
-FLOPS = 2 * 2 * B * N * D
-PE_SUMS = 5
+SCALED_ON_SCALAR = (0, 3, 5, 7)
+DOUBLED_ON_SCALAR = (0, 1, 2, 4)
 
 
 def tile_proto_metric_v_kernel(tc, x1, x2, grad_out, out_0, out_1):
     nc = tc.nc
-    x1_v = x1.rearrange("(g p j) d a b -> g p j (d a b)", p=P, j=4)
-    x2_v = x2.rearrange("(g p h e) s d a b -> g h p e s (d a b)", p=P, h=2, e=2)
-    go_v = grad_out.rearrange("(g p j) n -> g p j n", p=P, j=4)
-    o0_v = out_0.rearrange("(g p j) d a b -> g p j (d a b)", p=P, j=4)
-    o1_v = out_1.rearrange("(g p h e) s d a b -> g h p (e s) (d a b)", p=P, h=2, e=2)
+
+    grad_view = grad_out.rearrange("(b p j) n -> b p j n", p=P, j=SLOT)
+    x1_view = x1.rearrange("(b p j) d u v -> b p j (d u v)", p=P, j=SLOT)
+    x2_view = x2.rearrange("(h p half e) s d u v -> h half p e s (d u v)", p=P, half=2, e=2)
+    out_0_view = out_0.rearrange("(b p j) d u v -> b p j (d u v)", p=P, j=SLOT)
+    out_1_view = out_1.rearrange("(h p half e) s d u v -> h half p (e s) (d u v)", p=P, half=2, e=2)
 
     with ExitStack() as ctx:
         keep = ctx.enter_context(tc.tile_pool(name="keep", bufs=1))
         work = ctx.enter_context(tc.tile_pool(name="work", bufs=2))
         psum = ctx.enter_context(tc.psum_pool(name="psum", bufs=1))
 
-        ident_t = keep.tile([P, P], F32, name="ident_t", align_bytes=64)
-        make_identity(nc, ident_t[:])
-        ident = ident_t[:]
+        ident = keep.tile([P, P], F32, name="ident", align_bytes=64)
+        make_identity(nc, ident[:])
         ident_bf = keep.tile([P, P], BF16, name="ident_bf", align_bytes=64)
         make_identity(nc, ident_bf[:])
         ones = keep.tile([P, 2], BF16, name="ones")
         nc.vector.memset(ones[:], 1.0)
-        pick = keep.tile([P, 4, 4, 32], F32, name="pick", align_bytes=64)
+
+        pick = keep.tile([P, SLOT, 4, 32], F32, name="pick", align_bytes=64)
         nc.vector.tensor_copy(
             out=pick[:],
-            in_=ident.rearrange("p (q t) -> p t q", t=4).unsqueeze(2).to_broadcast([P, 4, 4, 32]),
+            in_=ident[:].rearrange("p (y t) -> p t y", t=SLOT).unsqueeze(2).to_broadcast([P, SLOT, 4, 32]),
         )
         quarter = keep.tile([P, 4], F32, name="quarter")
-        nc.vector.tensor_reduce(out=quarter[:], in_=ident.rearrange("p (k x) -> p k x", k=4), axis=AXIS_X, op=ADD)
+        nc.vector.tensor_reduce(out=quarter[:], in_=ident[:].rearrange("p (k y) -> p k y", k=4), axis=AXIS_X, op=ADD)
         mask = keep.tile([P, 4], F32, name="mask")
         nc.vector.tensor_scalar(
             out=mask[:], in0=quarter[:], scalar1=-2.0 / (SHOT * SHOT), scalar2=None, op0=MULT
         )
 
-        g_raw = [keep.tile([P, 4, N], BF16, name=f"g_raw{b}", align_bytes=64) for b in range(QP)]
-        q_raw = [keep.tile([P, 4, D], BF16, name=f"q_raw{b}", align_bytes=64) for b in range(QP)]
-        g_codes = [keep.tile([P, N], U32, name=f"g_codes{b}", align_bytes=64) for b in range(QP)]
-        g_scales = [keep.tile([P, N], U8, name=f"g_scales{b}", align_bytes=64) for b in range(QP)]
-        q_codes = [keep.tile([P, D], U32, name=f"q_codes{b}", align_bytes=64) for b in range(QP)]
-        q_scales = [keep.tile([P, D], U8, name=f"q_scales{b}", align_bytes=64) for b in range(QP)]
-        t_codes = [[keep.tile([P, PASS], U32, name=f"t_codes{h}_{b}", align_bytes=64) for b in range(QP)] for h in range(NP)]
-        t_scales = [[keep.tile([P, PASS], U8, name=f"t_scales{h}_{b}", align_bytes=64) for b in range(QP)] for h in range(NP)]
-        p_codes = [keep.tile([P, D], U32, name=f"p_codes{h}", align_bytes=64) for h in range(NP)]
-        p_scales = [keep.tile([P, D], U8, name=f"p_scales{h}", align_bytes=64) for h in range(NP)]
-        sums = [keep.tile([P, 4, D], F32, name=f"sums{h}", align_bytes=64) for h in range(NP)]
-        row_m2 = keep.tile([P, 4 * QP], F32, name="row_m2")
-        c_nat = keep.tile([P, N // P], F32, name="c_nat")
-        c_neg = keep.tile([P, 4, NP], F32, name="c_neg")
-        c_parts = psum.tile([P, 2 * QP, N // P], F32, name="c_parts", tag="c")
+        def keep_tiles(name, count, shape, dtype):
+            return [keep.tile(shape, dtype, name=f"{name}{k}", align_bytes=64) for k in range(count)]
 
-        x2_t = {}
-        gg, qg, gt, tp, acc, tmp, o0 = {}, {}, {}, {}, {}, {}, {}
-        s_ps, sv = {}, {}
+        grad_raw = keep_tiles("grad_raw", B_PASSES, [P, SLOT, N], BF16)
+        q_raw = keep_tiles("q_raw", B_PASSES, [P, SLOT, D], BF16)
+        grad_q_codes = keep_tiles("grad_q_codes", B_PASSES, [P, N], U32)
+        grad_q_scales = keep_tiles("grad_q_scales", B_PASSES, [P, N], U8)
+        q_codes = keep_tiles("q_codes", B_PASSES, [P, D], U32)
+        q_scales = keep_tiles("q_scales", B_PASSES, [P, D], U8)
+        grad_p_codes = [keep_tiles(f"grad_p_codes{h}_", B_PASSES, [P, PASS], U32) for h in range(N_PASSES)]
+        grad_p_scales = [keep_tiles(f"grad_p_scales{h}_", B_PASSES, [P, PASS], U8) for h in range(N_PASSES)]
+        p_codes = keep_tiles("p_codes", N_PASSES, [P, D], U32)
+        p_scales = keep_tiles("p_scales", N_PASSES, [P, D], U8)
+        shot_sums = keep_tiles("shot_sums", N_PASSES, [P, SLOT, D], F32)
+        row_factor = keep.tile([P, 4 * B_PASSES], F32, name="row_factor")
+        col_sum = keep.tile([P, N_BLOCKS], F32, name="col_sum")
+        col_masked = keep.tile([P, SLOT * N_PASSES, 4], F32, name="col_masked")
+        col_factor = keep.tile([P, SLOT, N_PASSES], F32, name="col_factor")
+        col_parts = psum.tile([P, 2 * B_PASSES, N_BLOCKS], F32, name="col_parts", tag="columns")
+        col_picked = {}
+
+        grouped_g, grouped_q, grouped_t, grouped_p = {}, {}, {}, {}
+        turned, shots, shot_bank, partial, scaled_sum, product, rows_0, rows_1 = {}, {}, {}, {}, {}, {}, {}, {}
+
 
         def load_x2(pair):
-            tile = work.tile([P, 2, SHOT, D], BF16, name="x2_pair", tag="big", bufs=4, align_bytes=64)
-            nc.sync.dma_start(out=tile[:], in_=x2_v[pair // 2, pair % 2])
-            for e in range(2):
-                x2_t[2 * pair + e] = tile[:, e, :, :]
+            shots[pair] = work.tile([P, 2, SHOT, D], BF16, name="x2_pair", tag="pair", bufs=4, align_bytes=64)
+            nc.sync.dma_start(out=shots[pair][:], in_=x2_view[pair // 2, pair % 2])
 
-        def transposes(b, m):
-            h, half = m // 2, m % 2
-            if half == 0:
-                gt[b, h] = work.tile([P, PASS, 4], BF16, name="gt", bufs=6, align_bytes=64)
-            bank = psum.tile([P, 2, 2, P], F32, name="bank", tag="x", bufs=4)
-            tp[b, m] = bank
-            for u in range(2):
-                for jj in range(2):
-                    words = g_raw[b][:, 2 * half + jj, PASS * h : PASS * (h + 1)].bitcast(F32)
-                    nc.tensor.transpose(bank[:, u, jj, :], words[:, u::2], ident)
 
-        def copy_t(b, m):
-            h, half = m // 2, m % 2
-            rows = gt[b, h][:].rearrange("p r t -> p (r t)").bitcast(F32)[:, 512 * half : 512 * (half + 1)]
-            nc.scalar.copy(
-                out=rows.rearrange("p (r u) -> p r u", u=2),
-                in_=tp[b, m][:].rearrange("p u j r -> p (j r) u"),
+        def quantise(codes, scales, grouped, fmt):
+            nc.vector.quantize_mx(
+                out=codes.bitcast(fmt), scales=scales, in_=grouped[:].rearrange("p c t -> p (c t)")
             )
 
-        def quant(codes, scales, src, fmt):
-            nc.vector.quantize_mx(out=codes.bitcast(fmt), scales=scales, in_=src[:].rearrange("p c t -> p (c t)"))
-
-        def quant_t(b, h):
-            quant(t_codes[h][b][:], t_scales[h][b][:], gt[b, h], E5M2)
-
-        def group_g(b, h, copy=nc.vector.tensor_copy):
-            gg[b, h] = work.tile([P, PASS, 4], BF16, name="gg", bufs=3, align_bytes=64)
+        def group_g(b, h, on_scalar=False):
+            grouped_g[b, h] = work.tile([P, PASS, SLOT], BF16, name="grouped_g", bufs=4, align_bytes=64)
+            copy = nc.scalar.copy if on_scalar else nc.vector.tensor_copy
             copy(
-                out=gg[b, h][:].rearrange("p (t c) j -> p c j t", t=4),
-                in_=g_raw[b][:, :, PASS * h : PASS * (h + 1)].rearrange("p j (c t) -> p c j t", t=4),
+                out=grouped_g[b, h][:].rearrange("p (t c) j -> p c j t", t=SLOT),
+                in_=grad_raw[b][:, :, PASS * h : PASS * (h + 1)].rearrange("p j (c t) -> p c j t", t=SLOT),
             )
 
-        def quant_g(b, h):
+        def quantise_g(b, h):
             cols = slice(PASS * h, PASS * (h + 1))
-            quant(g_codes[b][:, cols], g_scales[b][:, cols], gg[b, h], E5M2)
+            quantise(grad_q_codes[b][:, cols], grad_q_scales[b][:, cols], grouped_g[b, h], E5M2)
 
         def group_q(b):
-            qg[b] = work.tile([P, D, 4], BF16, name="qg", bufs=2, align_bytes=64)
+            grouped_q[b] = work.tile([P, D, SLOT], BF16, name="grouped_q", bufs=2, align_bytes=64)
             nc.scalar.copy(
-                out=qg[b][:].rearrange("p (d i) j -> p d j i", i=4),
-                in_=q_raw[b][:].rearrange("p j (d i) -> p d j i", i=4),
+                out=grouped_q[b][:].rearrange("p (d e) j -> p d j e", e=4),
+                in_=q_raw[b][:].rearrange("p j (d e) -> p d j e", e=4),
             )
 
-        def quant_q(b):
-            quant(q_codes[b][:], q_scales[b][:], qg[b], E4M3)
+        def quantise_q(b):
+            quantise(q_codes[b][:], q_scales[b][:], grouped_q[b], E4M3)
 
-        def col_sums(b):
+
+        def transpose(b, h, half):
+            if half == 0:
+                grouped_t[b, h] = work.tile([P, PASS, SLOT], BF16, name="grouped_t", bufs=6, align_bytes=64)
+            bank = psum.tile([P, 2, 2, P], F32, name="turned_bank", tag="bank", bufs=4)
+            turned[b, h, half] = bank
+            for u in range(2):
+                for e in range(2):
+                    words = grad_raw[b][:, 2 * half + e, PASS * h : PASS * (h + 1)].bitcast(F32)
+                    nc.tensor.transpose(bank[:, u, e, :], words[:, u::2], ident[:])
+
+        def copy_t(b, h, half):
+            words = grouped_t[b, h][:].rearrange("p q t -> p (q t)").bitcast(F32)
+            nc.scalar.copy(
+                out=words[:, 512 * half : 512 * (half + 1)].rearrange("p (q u) -> p q u", u=2),
+                in_=turned[b, h, half][:].rearrange("p u e q -> p (e q) u"),
+            )
+
+        def quantise_t(b, h):
+            quantise(grad_p_codes[h][b][:], grad_p_scales[h][b][:], grouped_t[b, h], E5M2)
+
+
+        def row_sum(i):
+            scratch = work.tile([P, N], BF16, name="scratch", bufs=2)
+            nc.scalar.activation(
+                out=scratch[:],
+                in_=grad_raw[i // 4][:, i % 4, :],
+                func=COPY,
+                scale=-2.0,
+                accum_out=row_factor[:, i : i + 1],
+            )
+
+        def column_parts(b):
             for half in range(2):
-                for k in range(N // P):
-                    for j in range(2):
+                for k in range(N_BLOCKS):
+                    for e in range(2):
                         nc.tensor.matmul(
-                            c_parts[:, 2 * b + half, k : k + 1],
-                            lhsT=g_raw[b][:, 2 * half + j, P * k : P * (k + 1)],
+                            col_parts[:, 2 * b + half, k : k + 1],
+                            lhsT=grad_raw[b][:, 2 * half + e, P * k : P * (k + 1)],
                             rhs=ones[:, 0:1],
-                            start=(j == 0),
-                            stop=(j == 1),
+                            start=(e == 0),
+                            stop=(e == 1),
                         )
 
-        def col_total():
-            nc.vector.tensor_reduce(out=c_nat[:], in_=c_parts[:].rearrange("p b k -> p k b"), axis=AXIS_X, op=ADD)
+        def add_columns():
+            nc.vector.tensor_reduce(out=col_sum[:], in_=col_parts[:].rearrange("p b k -> p k b"), axis=AXIS_X, op=ADD)
 
-        c_all = {}
-
-        def col_permute():
-            c_all[0] = psum.tile([P, 4, NP * 4], F32, name="c_perm", tag="c")
-            for t in range(4):
+        def permute_columns():
+            col_picked[0] = psum.tile([P, SLOT, N_BLOCKS], F32, name="col_picked", tag="columns")
+            for t in range(SLOT):
                 nc.tensor.matmul(
-                    c_all[0][:, t, :],
-                    lhsT=pick[:, t, :, :].rearrange("p r q -> p (r q)"),
-                    rhs=c_nat[:],
+                    col_picked[0][:, t, :],
+                    lhsT=pick[:, t, :, :].rearrange("p r y -> p (r y)"),
+                    rhs=col_sum[:],
                     start=True,
                     stop=True,
                 )
 
-        c_prod = keep.tile([P, 4 * NP, 4], F32, name="c_prod")
-
-        def col_mask():
+        def mask_columns():
             nc.vector.tensor_tensor(
-                out=c_prod[:],
-                in0=c_all[0][:].rearrange("p t (h k) -> p (t h) k", k=4),
-                in1=mask[:].unsqueeze(1).to_broadcast([P, 4 * NP, 4]),
+                out=col_masked[:],
+                in0=col_picked[0][:].rearrange("p t (h k) -> p (t h) k", k=4),
+                in1=mask[:].unsqueeze(1).to_broadcast([P, SLOT * N_PASSES, 4]),
                 op=MULT,
             )
 
-        def col_pick():
-            nc.vector.tensor_reduce(out=c_neg[:].rearrange("p t h -> p (t h)"), in_=c_prod[:], axis=AXIS_X, op=ADD)
-
-        def sum_pe(n):
-            s_ps[n] = psum.tile([P, D], F32, name="s_ps", tag="x", bufs=4)
-            for s in range(SHOT):
-                nc.tensor.matmul(s_ps[n][:], lhsT=ident_bf[:], rhs=x2_t[n][:, s, :], start=(s == 0), stop=(s == SHOT - 1))
-
-        def sum_copy(n):
-            nc.scalar.copy(out=sums[n // 4][:, n % 4, :], in_=s_ps[n][:])
-
-        def sum_v(n, part):
-            x = x2_t[n]
-            if part == 0:
-                sv[n] = (work.tile([P, D], F32, name="sum_a", bufs=1), work.tile([P, D], F32, name="sum_b", bufs=1))
-            a, b = sv[n]
-            if part == 0:
-                nc.vector.tensor_tensor(out=a[:], in0=x[:, 0, :], in1=x[:, 1, :], op=ADD)
-            if part == 1:
-                nc.vector.tensor_tensor(out=b[:], in0=x[:, 2, :], in1=x[:, 3, :], op=ADD)
-            if part == 2:
-                nc.vector.tensor_tensor(out=a[:], in0=a[:], in1=x[:, 4, :], op=ADD)
-            if part == 3:
-                nc.vector.tensor_tensor(out=sums[n // 4][:, n % 4, :], in0=a[:], in1=b[:], op=ADD)
-
-        def scaled(n):
-            tmp[n] = work.tile([P, D], F32, name="tmp", bufs=3)
-            nc.vector.tensor_scalar(
-                out=tmp[n][:], in0=sums[n // 4][:, n % 4, :], scalar1=c_neg[:, n % 4, n // 4 : n // 4 + 1], scalar2=None, op0=MULT
+        def pick_columns():
+            nc.vector.tensor_reduce(
+                out=col_factor[:].rearrange("p t h -> p (t h)"), in_=col_masked[:], axis=AXIS_X, op=ADD
             )
 
-        pg = {}
 
-        def group_p(h, scale=nc.vector.tensor_scalar_mul):
-            pg[h] = work.tile([P, D, 4], BF16, name="pg", bufs=1, align_bytes=64)
-            scale(pg[h][:], sums[h][:].rearrange("p j d -> p d j"), 2.0 / SHOT)
+        def shot(n, s):
+            return shots[n // 2][:, n % 2, s, :]
 
-        def quant_p(h):
-            quant(p_codes[h][:], p_scales[h][:], pg[h], E4M3)
+        def sum_on_tensor(n):
+            shot_bank[n] = psum.tile([P, D], F32, name="shot_bank", tag="bank", bufs=4)
+            for s in range(SHOT):
+                nc.tensor.matmul(shot_bank[n][:], lhsT=ident_bf[:], rhs=shot(n, s), start=(s == 0), stop=(s == SHOT - 1))
 
-        def mm_q(n):
-            acc["q", n] = psum.tile([P, D], F32, name="acc_q", tag="acc", bufs=3)
+        def copy_sum(n):
+            nc.scalar.copy(out=shot_sums[n // 4][:, n % 4, :], in_=shot_bank[n][:])
+
+        def sum_on_vector(n, step):
+            if step == 0:
+                partial[0] = work.tile([P, D], F32, name="partial_0", bufs=1)
+                partial[1] = work.tile([P, D], F32, name="partial_1", bufs=1)
+            out, in0, in1 = (
+                (partial[0][:], shot(n, 0), shot(n, 1)),
+                (partial[1][:], shot(n, 2), shot(n, 3)),
+                (partial[0][:], partial[0][:], shot(n, 4)),
+                (shot_sums[n // 4][:, n % 4, :], partial[0][:], partial[1][:]),
+            )[step]
+            nc.vector.tensor_tensor(out=out, in0=in0, in1=in1, op=ADD)
+
+        def group_p(h):
+            grouped_p[h] = work.tile([P, D, SLOT], BF16, name="grouped_p", bufs=1, align_bytes=64)
+            nc.vector.tensor_scalar_mul(grouped_p[h][:], shot_sums[h][:].rearrange("p j d -> p d j"), 2.0 / SHOT)
+
+        def quantise_p(h):
+            quantise(p_codes[h][:], p_scales[h][:], grouped_p[h], E4M3)
+
+
+        def scale_sum(n):
+            scaled_sum[n] = work.tile([P, D], F32, name="scaled_sum", bufs=3)
+            source, factor = shot_sums[n // 4][:, n % 4, :], col_factor[:, n % 4, n // 4 : n // 4 + 1]
+            if n in SCALED_ON_SCALAR:
+                nc.scalar.activation(out=scaled_sum[n][:], in_=source, func=COPY, scale=factor)
+            else:
+                nc.vector.tensor_scalar(out=scaled_sum[n][:], in0=source, scalar1=factor, scalar2=None, op0=MULT)
+
+        def multiply_1(n):
+            product[1, n] = psum.tile([P, D], F32, name="product_1", tag="product", bufs=3)
             cols = slice(P * n, P * (n + 1))
-            for b in range(QP):
+            for b in range(B_PASSES):
                 nc.tensor.matmul_mx(
-                    out=acc["q", n][:],
-                    lhsT=g_codes[b][:, cols].bitcast(E5M2),
-                    lhsT_scale=g_scales[b][:, cols],
+                    out=product[1, n][:],
+                    lhsT=grad_q_codes[b][:, cols].bitcast(E5M2),
+                    lhsT_scale=grad_q_scales[b][:, cols],
                     rhs=q_codes[b][:].bitcast(E4M3),
                     rhs_scale=q_scales[b][:],
                     start=(b == 0),
-                    stop=(b == QP - 1),
+                    stop=(b == B_PASSES - 1),
                 )
 
-        o1 = {}
-
         def finish_1(n):
-            pair, e = n // 2, n % 2
-            if e == 0:
-                o1[pair] = work.tile([P, 4, D], F32, name="o1", tag="big", bufs=4, align_bytes=64)
+            if n % 2 == 0:
+                rows_1[n // 2] = work.tile([P, 4, D], F32, name="rows_1", tag="pair", bufs=4, align_bytes=64)
             nc.vector.scalar_tensor_tensor(
-                out=o1[pair][:, 2 * e, :], in0=acc["q", n][:], scalar=2.0 / SHOT, in1=tmp[n][:], op0=MULT, op1=ADD
+                out=rows_1[n // 2][:, 2 * (n % 2), :],
+                in0=product[1, n][:],
+                scalar=2.0 / SHOT,
+                in1=scaled_sum[n][:],
+                op0=MULT,
+                op1=ADD,
             )
 
-        def send_1(n):
-            pair, e = n // 2, n % 2
-            dst = o1_v[pair // 2, pair % 2]
-            src = o1[pair]
-            nc.vector.tensor_copy(out=src[:, 2 * e + 1, :], in_=src[:, 2 * e, :])
-            if e == 1:
+        def double_1(n):
+            row = 2 * (n % 2)
+            copy = nc.scalar.copy if n in DOUBLED_ON_SCALAR else nc.vector.tensor_copy
+            copy(out=rows_1[n // 2][:, row + 1, :], in_=rows_1[n // 2][:, row, :])
+
+        def store_1(n):
+            dst, src = out_1_view[n // 4, n % 4 // 2], rows_1[n // 2]
+            if n == 0:
+                nc.sync.dma_start(out=dst[:, 0:4, :], in_=src[:, 0, :].unsqueeze(1).to_broadcast([P, 4, D]))
+                return
+            if n % 2 == 1:
                 nc.sync.dma_start(out=dst[:, 4:6, :], in_=src[:, 1:3, :])
-            rows = dst[:, 6 * e : 6 * e + 4, :].rearrange("p (r s) d -> p r (s d)", s=2)
+            first, row = 6 * (n % 2), 2 * (n % 2)
             nc.sync.dma_start(
-                out=rows,
-                in_=src[:, 2 * e : 2 * e + 2, :].rearrange("p s d -> p (s d)").unsqueeze(1).to_broadcast([P, 2, 2 * D]),
+                out=dst[:, first : first + 4, :].rearrange("p (r s) d -> p r (s d)", s=2),
+                in_=src[:, row : row + 2, :].rearrange("p s d -> p (s d)").unsqueeze(1).to_broadcast([P, 2, 2 * D]),
             )
 
-        def row_sum(i):
-            dump = work.tile([P, N], BF16, name="dump", bufs=2)
-            nc.scalar.activation(
-                out=dump[:], in_=g_raw[i // 4][:, i % 4, :], func=COPY, scale=-2.0, accum_out=row_m2[:, i : i + 1]
-            )
 
-        def mm_p(i):
+        def multiply_0(i):
             b, j = i // 4, i % 4
-            acc["p", i] = psum.tile([P, D], F32, name="acc_p", tag="acc", bufs=3)
+            product[0, i] = psum.tile([P, D], F32, name="product_0", tag="product", bufs=3)
             cols = slice(P * j, P * (j + 1))
-            for h in range(NP):
+            for h in range(N_PASSES):
                 nc.tensor.matmul_mx(
-                    out=acc["p", i][:],
-                    lhsT=t_codes[h][b][:, cols].bitcast(E5M2),
-                    lhsT_scale=t_scales[h][b][:, cols],
+                    out=product[0, i][:],
+                    lhsT=grad_p_codes[h][b][:, cols].bitcast(E5M2),
+                    lhsT_scale=grad_p_scales[h][b][:, cols],
                     rhs=p_codes[h][:].bitcast(E4M3),
                     rhs_scale=p_scales[h][:],
                     start=(h == 0),
-                    stop=(h == NP - 1),
+                    stop=(h == N_PASSES - 1),
                 )
 
         def finish_0(i):
             b, j = i // 4, i % 4
             if j == 0:
-                o0[b] = work.tile([P, 4, D], F32, name="o0", tag="big", bufs=4, align_bytes=64)
+                rows_0[b] = work.tile([P, SLOT, D], F32, name="rows_0", tag="pair", bufs=4, align_bytes=64)
             nc.vector.scalar_tensor_tensor(
-                out=o0[b][:, j, :], in0=q_raw[b][:, j, :], scalar=row_m2[:, i : i + 1], in1=acc["p", i][:], op0=MULT, op1=ADD
+                out=rows_0[b][:, j, :],
+                in0=q_raw[b][:, j, :],
+                scalar=row_factor[:, i : i + 1],
+                in1=product[0, i][:],
+                op0=MULT,
+                op1=ADD,
             )
-            cut = {3: 0} if b == 0 else {1: 0, 3: 2}
-            if j in cut:
-                nc.sync.dma_start(out=o0_v[b, :, cut[j] : j + 1, :], in_=o0[b][:, cut[j] : j + 1, :])
+            width = SLOT if b == 0 else 2
+            if (j + 1) % width == 0:
+                nc.sync.dma_start(
+                    out=out_0_view[b, :, j + 1 - width : j + 1, :], in_=rows_0[b][:, j + 1 - width : j + 1, :]
+                )
 
         with tc.manual_schedule():
             for half in range(2):
-                nc.sync.dma_start(out=g_raw[0][:, 2 * half : 2 * half + 2, :], in_=go_v[0, :, 2 * half : 2 * half + 2, :])
-            nc.sync.dma_start(out=q_raw[0][:], in_=x1_v[0])
-            for b in range(1, QP):
-                nc.sync.dma_start(out=g_raw[b][:], in_=go_v[b])
-                nc.sync.dma_start(out=q_raw[b][:], in_=x1_v[b])
+                slots = slice(2 * half, 2 * half + 2)
+                nc.sync.dma_start(out=grad_raw[0][:, slots, :], in_=grad_view[0, :, slots, :])
+            nc.sync.dma_start(out=q_raw[0][:], in_=x1_view[0])
+            for b in range(1, B_PASSES):
+                nc.sync.dma_start(out=grad_raw[b][:], in_=grad_view[b])
+                nc.sync.dma_start(out=q_raw[b][:], in_=x1_view[b])
             for pair in range(4):
                 load_x2(pair)
 
-            def T(*banks):
-                for b, m in banks:
-                    transposes(b, m)
-                for b, m in banks:
-                    copy_t(b, m)
-
             row_sum(0)
             row_sum(1)
-            col_sums(0)
-            group_g(0, 0)
-            group_q(0)
-            group_g(0, 1)
-            quant_g(0, 0)
-            transposes(0, 0)
-            transposes(0, 1)
-            col_sums(1)
-            group_g(1, 0)
-            quant_g(0, 1)
-            group_g(1, 1, nc.scalar.copy)
-            quant_q(0)
-            group_q(1)
-            quant_g(1, 0)
-            quant_g(1, 1)
-            col_sums(2)
-            group_g(2, 0)
-            group_g(2, 1, nc.scalar.copy)
-            quant_q(1)
-            quant_g(2, 0)
-            group_q(2)
-            col_sums(3)
-            group_g(3, 0)
-            quant_g(2, 1)
-            group_q(3)
-            group_g(3, 1)
-            quant_q(2)
-            quant_g(3, 0)
-            sum_pe(0)
-            copy_t(0, 0)
-            copy_t(0, 1)
-            sum_copy(0)
-            quant_g(3, 1)
-            col_total()
-            col_permute()
-            quant_q(3)
-            mm_q(0)
+            for b in range(B_PASSES):
+                column_parts(b)
+                if b < 2:
+                    transpose(0, 0, b)
+                if b == 2:
+                    group_g(b, 1, on_scalar=True)
+                group_q(b)
+                if b == 0:
+                    row_sum(2)
+                group_g(b, 0)
+                if b != 2:
+                    group_g(b, 1)
+                quantise_g(b, 0)
+                if b > 0:
+                    quantise_g(b - 1, 1)
+                    quantise_q(b - 1)
+
+            add_columns()
+            sum_on_tensor(0)
+            copy_sum(0)
+            quantise_q(3)
+            permute_columns()
+            sum_on_vector(1, 0)
+            mask_columns()
+            sum_on_vector(1, 1)
+            pick_columns()
             row_sum(3)
-            sum_v(1, 0)
-            col_mask()
-            sum_v(1, 1)
-            col_pick()
-            sum_v(1, 2)
-            scaled(0)
-            sum_v(1, 3)
-            sum_pe(2)
-            sum_copy(2)
+            scale_sum(0)
+            multiply_1(0)
+            multiply_1(1)
+            copy_t(0, 0, 0)
+            sum_on_vector(1, 2)
             finish_1(0)
-            mm_q(1)
-            scaled(1)
-            send_1(0)
-            sum_pe(3)
-            row_sum(4)
-            sum_copy(3)
+            store_1(0)
+
+            sum_on_tensor(2)
+            sum_on_vector(1, 3)
+            scale_sum(1)
+            copy_t(0, 0, 1)
+            double_1(0)
+            sum_on_vector(5, 0)
             finish_1(1)
-            mm_q(2)
-            scaled(2)
-            sum_v(5, 0)
-            send_1(1)
-            row_sum(2)
-            row_sum(5)
-            T((0, 2), (0, 3))
-            mm_q(3)
+            copy_sum(2)
+            double_1(1)
+            store_1(1)
+
+            multiply_1(2)
+            scale_sum(2)
+            sum_on_vector(5, 1)
+            sum_on_vector(5, 2)
+            sum_on_tensor(3)
+            copy_sum(3)
             finish_1(2)
-            scaled(3)
-            send_1(2)
-            sum_v(5, 1)
-            sum_v(5, 2)
-            sum_pe(4)
+            double_1(2)
+            store_1(2)
+
+            multiply_1(3)
+            sum_on_vector(5, 3)
+            sum_on_vector(7, 0)
+            scale_sum(3)
             finish_1(3)
-            row_sum(6)
-            sum_copy(4)
-            sum_v(5, 3)
-            send_1(3)
-            mm_q(4)
-            row_sum(7)
-            T((1, 0), (1, 1))
+            transpose(0, 1, 0)
+            transpose(0, 1, 1)
+            copy_t(0, 1, 0)
+            transpose(1, 0, 0)
+            quantise_g(3, 1)
+            double_1(3)
+            store_1(3)
+
+            row_sum(4)
+            copy_t(0, 1, 1)
+            sum_on_tensor(4)
+            copy_sum(4)
+            multiply_1(4)
+            quantise_t(0, 0)
             group_p(0)
-            scaled(4)
-            scaled(5)
+            scale_sum(4)
+            quantise_t(0, 1)
             finish_1(4)
-            mm_q(5)
-            sum_v(7, 0)
-            send_1(4)
-            row_sum(8)
-            T((1, 2), (1, 3))
-            sum_pe(6)
+            transpose(1, 0, 1)
+            transpose(1, 1, 0)
+            copy_t(1, 0, 0)
+            transpose(1, 1, 1)
+            row_sum(5)
+            copy_t(1, 0, 1)
+            scale_sum(5)
+            double_1(4)
+            store_1(4)
+
+            copy_t(1, 1, 0)
+            copy_t(1, 1, 1)
+            multiply_1(5)
+            sum_on_tensor(6)
+            copy_sum(6)
+            sum_on_vector(7, 1)
+            sum_on_vector(7, 2)
             finish_1(5)
-            row_sum(9)
-            sum_copy(6)
-            sum_v(7, 1)
-            send_1(5)
-            quant_p(0)
-            T((2, 0), (2, 1))
-            sum_v(7, 2)
-            quant_t(0, 0)
-            scaled(6)
-            sum_v(7, 3)
-            mm_q(6)
-            quant_t(0, 1)
+            quantise_p(0)
+            double_1(5)
+            store_1(5)
+
+            multiply_1(6)
+            transpose(2, 0, 0)
+            transpose(2, 0, 1)
+            row_sum(6)
+            scale_sum(6)
+            sum_on_vector(7, 3)
+            scale_sum(7)
             finish_1(6)
-            scaled(7)
-            send_1(6)
-            mm_q(7)
-            row_sum(10)
-            group_p(1, nc.scalar.mul)
-            T((2, 2), (2, 3))
+            quantise_t(1, 0)
+            group_p(1)
+            double_1(6)
+            store_1(6)
+
+            multiply_1(7)
             finish_1(7)
-            quant_t(1, 0)
-            send_1(7)
-            quant_t(1, 1)
-            quant_p(1)
-            for i in range(16):
-                if i == 2:
-                    T((3, 0), (3, 1))
-                if i == 5:
-                    T((3, 2), (3, 3))
-                if i == 3:
-                    quant_t(2, 0)
-                if i == 5:
-                    quant_t(2, 1)
-                if i == 8:
-                    quant_t(3, 0)
-                if i == 10:
-                    quant_t(3, 1)
-                mm_p(i)
-                if 3 <= i < 8:
-                    row_sum(i + 8)
+            row_sum(7)
+            copy_t(2, 0, 0)
+            copy_t(2, 0, 1)
+            transpose(2, 1, 0)
+            quantise_t(1, 1)
+            quantise_p(1)
+            quantise_t(2, 0)
+            double_1(7)
+            store_1(7)
+
+            transpose(2, 1, 1)
+            copy_t(2, 1, 0)
+            copy_t(2, 1, 1)
+            for half in range(2):
+                transpose(3, 0, half)
+                copy_t(3, 0, half)
+            transpose(3, 1, 0)
+            row_sum(8)
+            copy_t(3, 1, 0)
+            for i in range(4 * B_PASSES):
+                multiply_0(i)
                 finish_0(i)
+                if i < 3:
+                    row_sum(9 + i)
+                if i == 4:
+                    quantise_t(2, 1)
+                if i == 6:
+                    quantise_t(3, 0)
+                if i == 7:
+                    transpose(3, 1, 1)
+                    copy_t(3, 1, 1)
+                if 8 <= i < 12:
+                    row_sum(4 + i)
+                if i == 9:
+                    quantise_t(3, 1)

from contextlib import ExitStack

import concourse.mybir as mybir
from concourse.masks import make_identity

B, N, SHOT, D = 2048, 1024, 5, 512
FLOPS = 2 * 2 * B * N * D

F32 = mybir.dt.float32
BF16 = mybir.dt.bfloat16
U32 = mybir.dt.uint32
U8 = mybir.dt.uint8
E4M3 = mybir.dt.float8_e4m3fn_x4
E5M2 = mybir.dt.float8_e5m2_x4
COPY = mybir.ActivationFunctionType.Copy
ADD = mybir.AluOpType.add
MULT = mybir.AluOpType.mult
AXIS_X = mybir.AxisListType.X

P = 128
SLOT = 4
PASS = P * SLOT
B_PASSES = B // PASS
N_PASSES = N // PASS
N_BLOCKS = N // P

SCALED_ON_SCALAR = (0, 3, 5, 7)
DOUBLED_ON_SCALAR = (0, 1, 2, 4)


def tile_proto_metric_v_kernel(tc, x1, x2, grad_out, out_0, out_1):
    nc = tc.nc

    grad_view = grad_out.rearrange("(b p j) n -> b p j n", p=P, j=SLOT)
    x1_view = x1.rearrange("(b p j) d u v -> b p j (d u v)", p=P, j=SLOT)
    x2_view = x2.rearrange("(h p half e) s d u v -> h half p e s (d u v)", p=P, half=2, e=2)
    out_0_view = out_0.rearrange("(b p j) d u v -> b p j (d u v)", p=P, j=SLOT)
    out_1_view = out_1.rearrange("(h p half e) s d u v -> h half p (e s) (d u v)", p=P, half=2, e=2)

    with ExitStack() as ctx:
        keep = ctx.enter_context(tc.tile_pool(name="keep", bufs=1))
        work = ctx.enter_context(tc.tile_pool(name="work", bufs=2))
        psum = ctx.enter_context(tc.psum_pool(name="psum", bufs=1))

        ident = keep.tile([P, P], F32, name="ident", align_bytes=64)
        make_identity(nc, ident[:])
        ident_bf = keep.tile([P, P], BF16, name="ident_bf", align_bytes=64)
        make_identity(nc, ident_bf[:])
        ones = keep.tile([P, 2], BF16, name="ones")
        nc.vector.memset(ones[:], 1.0)

        pick = keep.tile([P, SLOT, 4, 32], F32, name="pick", align_bytes=64)
        nc.vector.tensor_copy(
            out=pick[:],
            in_=ident[:].rearrange("p (y t) -> p t y", t=SLOT).unsqueeze(2).to_broadcast([P, SLOT, 4, 32]),
        )
        quarter = keep.tile([P, 4], F32, name="quarter")
        nc.vector.tensor_reduce(out=quarter[:], in_=ident[:].rearrange("p (k y) -> p k y", k=4), axis=AXIS_X, op=ADD)
        mask = keep.tile([P, 4], F32, name="mask")
        nc.vector.tensor_scalar(
            out=mask[:], in0=quarter[:], scalar1=-2.0 / (SHOT * SHOT), scalar2=None, op0=MULT
        )

        def keep_tiles(name, count, shape, dtype):
            return [keep.tile(shape, dtype, name=f"{name}{k}", align_bytes=64) for k in range(count)]

        grad_raw = keep_tiles("grad_raw", B_PASSES, [P, SLOT, N], BF16)
        q_raw = keep_tiles("q_raw", B_PASSES, [P, SLOT, D], BF16)
        grad_q_codes = keep_tiles("grad_q_codes", B_PASSES, [P, N], U32)
        grad_q_scales = keep_tiles("grad_q_scales", B_PASSES, [P, N], U8)
        q_codes = keep_tiles("q_codes", B_PASSES, [P, D], U32)
        q_scales = keep_tiles("q_scales", B_PASSES, [P, D], U8)
        grad_p_codes = [keep_tiles(f"grad_p_codes{h}_", B_PASSES, [P, PASS], U32) for h in range(N_PASSES)]
        grad_p_scales = [keep_tiles(f"grad_p_scales{h}_", B_PASSES, [P, PASS], U8) for h in range(N_PASSES)]
        p_codes = keep_tiles("p_codes", N_PASSES, [P, D], U32)
        p_scales = keep_tiles("p_scales", N_PASSES, [P, D], U8)
        shot_sums = keep_tiles("shot_sums", N_PASSES, [P, SLOT, D], F32)
        row_factor = keep.tile([P, 4 * B_PASSES], F32, name="row_factor")
        col_sum = keep.tile([P, N_BLOCKS], F32, name="col_sum")
        col_masked = keep.tile([P, SLOT * N_PASSES, 4], F32, name="col_masked")
        col_factor = keep.tile([P, SLOT, N_PASSES], F32, name="col_factor")
        col_parts = psum.tile([P, 2 * B_PASSES, N_BLOCKS], F32, name="col_parts", tag="columns")
        col_picked = {}

        grouped_g, grouped_q, grouped_t, grouped_p = {}, {}, {}, {}
        turned, shots, shot_bank, partial, scaled_sum, product, rows_0, rows_1 = {}, {}, {}, {}, {}, {}, {}, {}


        def load_x2(pair):
            shots[pair] = work.tile([P, 2, SHOT, D], BF16, name="x2_pair", tag="pair", bufs=4, align_bytes=64)
            nc.sync.dma_start(out=shots[pair][:], in_=x2_view[pair // 2, pair % 2])


        def quantise(codes, scales, grouped, fmt):
            nc.vector.quantize_mx(
                out=codes.bitcast(fmt), scales=scales, in_=grouped[:].rearrange("p c t -> p (c t)")
            )

        def group_g(b, h, on_scalar=False):
            grouped_g[b, h] = work.tile([P, PASS, SLOT], BF16, name="grouped_g", bufs=4, align_bytes=64)
            copy = nc.scalar.copy if on_scalar else nc.vector.tensor_copy
            copy(
                out=grouped_g[b, h][:].rearrange("p (t c) j -> p c j t", t=SLOT),
                in_=grad_raw[b][:, :, PASS * h : PASS * (h + 1)].rearrange("p j (c t) -> p c j t", t=SLOT),
            )

        def quantise_g(b, h):
            cols = slice(PASS * h, PASS * (h + 1))
            quantise(grad_q_codes[b][:, cols], grad_q_scales[b][:, cols], grouped_g[b, h], E5M2)

        def group_q(b):
            grouped_q[b] = work.tile([P, D, SLOT], BF16, name="grouped_q", bufs=2, align_bytes=64)
            nc.scalar.copy(
                out=grouped_q[b][:].rearrange("p (d e) j -> p d j e", e=4),
                in_=q_raw[b][:].rearrange("p j (d e) -> p d j e", e=4),
            )

        def quantise_q(b):
            quantise(q_codes[b][:], q_scales[b][:], grouped_q[b], E4M3)


        def transpose(b, h, half):
            if half == 0:
                grouped_t[b, h] = work.tile([P, PASS, SLOT], BF16, name="grouped_t", bufs=6, align_bytes=64)
            bank = psum.tile([P, 2, 2, P], F32, name="turned_bank", tag="bank", bufs=4)
            turned[b, h, half] = bank
            for u in range(2):
                for e in range(2):
                    words = grad_raw[b][:, 2 * half + e, PASS * h : PASS * (h + 1)].bitcast(F32)
                    nc.tensor.transpose(bank[:, u, e, :], words[:, u::2], ident[:])

        def copy_t(b, h, half):
            words = grouped_t[b, h][:].rearrange("p q t -> p (q t)").bitcast(F32)
            nc.scalar.copy(
                out=words[:, 512 * half : 512 * (half + 1)].rearrange("p (q u) -> p q u", u=2),
                in_=turned[b, h, half][:].rearrange("p u e q -> p (e q) u"),
            )

        def quantise_t(b, h):
            quantise(grad_p_codes[h][b][:], grad_p_scales[h][b][:], grouped_t[b, h], E5M2)


        def row_sum(i):
            scratch = work.tile([P, N], BF16, name="scratch", bufs=2)
            nc.scalar.activation(
                out=scratch[:],
                in_=grad_raw[i // 4][:, i % 4, :],
                func=COPY,
                scale=-2.0,
                accum_out=row_factor[:, i : i + 1],
            )

        def column_parts(b):
            for half in range(2):
                for k in range(N_BLOCKS):
                    for e in range(2):
                        nc.tensor.matmul(
                            col_parts[:, 2 * b + half, k : k + 1],
                            lhsT=grad_raw[b][:, 2 * half + e, P * k : P * (k + 1)],
                            rhs=ones[:, 0:1],
                            start=(e == 0),
                            stop=(e == 1),
                        )

        def add_columns():
            nc.vector.tensor_reduce(out=col_sum[:], in_=col_parts[:].rearrange("p b k -> p k b"), axis=AXIS_X, op=ADD)

        def permute_columns():
            col_picked[0] = psum.tile([P, SLOT, N_BLOCKS], F32, name="col_picked", tag="columns")
            for t in range(SLOT):
                nc.tensor.matmul(
                    col_picked[0][:, t, :],
                    lhsT=pick[:, t, :, :].rearrange("p r y -> p (r y)"),
                    rhs=col_sum[:],
                    start=True,
                    stop=True,
                )

        def mask_columns():
            nc.vector.tensor_tensor(
                out=col_masked[:],
                in0=col_picked[0][:].rearrange("p t (h k) -> p (t h) k", k=4),
                in1=mask[:].unsqueeze(1).to_broadcast([P, SLOT * N_PASSES, 4]),
                op=MULT,
            )

        def pick_columns():
            nc.vector.tensor_reduce(
                out=col_factor[:].rearrange("p t h -> p (t h)"), in_=col_masked[:], axis=AXIS_X, op=ADD
            )


        def shot(n, s):
            return shots[n // 2][:, n % 2, s, :]

        def sum_on_tensor(n):
            shot_bank[n] = psum.tile([P, D], F32, name="shot_bank", tag="bank", bufs=4)
            for s in range(SHOT):
                nc.tensor.matmul(shot_bank[n][:], lhsT=ident_bf[:], rhs=shot(n, s), start=(s == 0), stop=(s == SHOT - 1))

        def copy_sum(n):
            nc.scalar.copy(out=shot_sums[n // 4][:, n % 4, :], in_=shot_bank[n][:])

        def sum_on_vector(n, step):
            if step == 0:
                partial[0] = work.tile([P, D], F32, name="partial_0", bufs=1)
                partial[1] = work.tile([P, D], F32, name="partial_1", bufs=1)
            out, in0, in1 = (
                (partial[0][:], shot(n, 0), shot(n, 1)),
                (partial[1][:], shot(n, 2), shot(n, 3)),
                (partial[0][:], partial[0][:], shot(n, 4)),
                (shot_sums[n // 4][:, n % 4, :], partial[0][:], partial[1][:]),
            )[step]
            nc.vector.tensor_tensor(out=out, in0=in0, in1=in1, op=ADD)

        def group_p(h):
            grouped_p[h] = work.tile([P, D, SLOT], BF16, name="grouped_p", bufs=1, align_bytes=64)
            nc.vector.tensor_scalar_mul(grouped_p[h][:], shot_sums[h][:].rearrange("p j d -> p d j"), 2.0 / SHOT)

        def quantise_p(h):
            quantise(p_codes[h][:], p_scales[h][:], grouped_p[h], E4M3)


        def scale_sum(n):
            scaled_sum[n] = work.tile([P, D], F32, name="scaled_sum", bufs=3)
            source, factor = shot_sums[n // 4][:, n % 4, :], col_factor[:, n % 4, n // 4 : n // 4 + 1]
            if n in SCALED_ON_SCALAR:
                nc.scalar.activation(out=scaled_sum[n][:], in_=source, func=COPY, scale=factor)
            else:
                nc.vector.tensor_scalar(out=scaled_sum[n][:], in0=source, scalar1=factor, scalar2=None, op0=MULT)

        def multiply_1(n):
            product[1, n] = psum.tile([P, D], F32, name="product_1", tag="product", bufs=3)
            cols = slice(P * n, P * (n + 1))
            for b in range(B_PASSES):
                nc.tensor.matmul_mx(
                    out=product[1, n][:],
                    lhsT=grad_q_codes[b][:, cols].bitcast(E5M2),
                    lhsT_scale=grad_q_scales[b][:, cols],
                    rhs=q_codes[b][:].bitcast(E4M3),
                    rhs_scale=q_scales[b][:],
                    start=(b == 0),
                    stop=(b == B_PASSES - 1),
                )

        def finish_1(n):
            if n % 2 == 0:
                rows_1[n // 2] = work.tile([P, 4, D], F32, name="rows_1", tag="pair", bufs=4, align_bytes=64)
            nc.vector.scalar_tensor_tensor(
                out=rows_1[n // 2][:, 2 * (n % 2), :],
                in0=product[1, n][:],
                scalar=2.0 / SHOT,
                in1=scaled_sum[n][:],
                op0=MULT,
                op1=ADD,
            )

        def double_1(n):
            row = 2 * (n % 2)
            copy = nc.scalar.copy if n in DOUBLED_ON_SCALAR else nc.vector.tensor_copy
            copy(out=rows_1[n // 2][:, row + 1, :], in_=rows_1[n // 2][:, row, :])

        def store_1(n):
            dst, src = out_1_view[n // 4, n % 4 // 2], rows_1[n // 2]
            if n == 0:
                nc.sync.dma_start(out=dst[:, 0:4, :], in_=src[:, 0, :].unsqueeze(1).to_broadcast([P, 4, D]))
                return
            if n % 2 == 1:
                nc.sync.dma_start(out=dst[:, 4:6, :], in_=src[:, 1:3, :])
            first, row = 6 * (n % 2), 2 * (n % 2)
            nc.sync.dma_start(
                out=dst[:, first : first + 4, :].rearrange("p (r s) d -> p r (s d)", s=2),
                in_=src[:, row : row + 2, :].rearrange("p s d -> p (s d)").unsqueeze(1).to_broadcast([P, 2, 2 * D]),
            )


        def multiply_0(i):
            b, j = i // 4, i % 4
            product[0, i] = psum.tile([P, D], F32, name="product_0", tag="product", bufs=3)
            cols = slice(P * j, P * (j + 1))
            for h in range(N_PASSES):
                nc.tensor.matmul_mx(
                    out=product[0, i][:],
                    lhsT=grad_p_codes[h][b][:, cols].bitcast(E5M2),
                    lhsT_scale=grad_p_scales[h][b][:, cols],
                    rhs=p_codes[h][:].bitcast(E4M3),
                    rhs_scale=p_scales[h][:],
                    start=(h == 0),
                    stop=(h == N_PASSES - 1),
                )

        def finish_0(i):
            b, j = i // 4, i % 4
            if j == 0:
                rows_0[b] = work.tile([P, SLOT, D], F32, name="rows_0", tag="pair", bufs=4, align_bytes=64)
            nc.vector.scalar_tensor_tensor(
                out=rows_0[b][:, j, :],
                in0=q_raw[b][:, j, :],
                scalar=row_factor[:, i : i + 1],
                in1=product[0, i][:],
                op0=MULT,
                op1=ADD,
            )
            width = SLOT if b == 0 else 2
            if (j + 1) % width == 0:
                nc.sync.dma_start(
                    out=out_0_view[b, :, j + 1 - width : j + 1, :], in_=rows_0[b][:, j + 1 - width : j + 1, :]
                )

        with tc.manual_schedule():
            for half in range(2):
                slots = slice(2 * half, 2 * half + 2)
                nc.sync.dma_start(out=grad_raw[0][:, slots, :], in_=grad_view[0, :, slots, :])
            nc.sync.dma_start(out=q_raw[0][:], in_=x1_view[0])
            for b in range(1, B_PASSES):
                nc.sync.dma_start(out=grad_raw[b][:], in_=grad_view[b])
                nc.sync.dma_start(out=q_raw[b][:], in_=x1_view[b])
            for pair in range(4):
                load_x2(pair)

            row_sum(0)
            row_sum(1)
            for b in range(B_PASSES):
                column_parts(b)
                if b < 2:
                    transpose(0, 0, b)
                if b == 2:
                    group_g(b, 1, on_scalar=True)
                group_q(b)
                if b == 0:
                    row_sum(2)
                group_g(b, 0)
                if b != 2:
                    group_g(b, 1)
                quantise_g(b, 0)
                if b > 0:
                    quantise_g(b - 1, 1)
                    quantise_q(b - 1)

            add_columns()
            sum_on_tensor(0)
            copy_sum(0)
            quantise_q(3)
            permute_columns()
            sum_on_vector(1, 0)
            mask_columns()
            sum_on_vector(1, 1)
            pick_columns()
            row_sum(3)
            scale_sum(0)
            multiply_1(0)
            multiply_1(1)
            copy_t(0, 0, 0)
            sum_on_vector(1, 2)
            finish_1(0)
            store_1(0)

            sum_on_tensor(2)
            sum_on_vector(1, 3)
            scale_sum(1)
            copy_t(0, 0, 1)
            double_1(0)
            sum_on_vector(5, 0)
            finish_1(1)
            copy_sum(2)
            double_1(1)
            store_1(1)

            multiply_1(2)
            scale_sum(2)
            sum_on_vector(5, 1)
            sum_on_vector(5, 2)
            sum_on_tensor(3)
            copy_sum(3)
            finish_1(2)
            double_1(2)
            store_1(2)

            multiply_1(3)
            sum_on_vector(5, 3)
            sum_on_vector(7, 0)
            scale_sum(3)
            finish_1(3)
            transpose(0, 1, 0)
            transpose(0, 1, 1)
            copy_t(0, 1, 0)
            transpose(1, 0, 0)
            quantise_g(3, 1)
            double_1(3)
            store_1(3)

            row_sum(4)
            copy_t(0, 1, 1)
            sum_on_tensor(4)
            copy_sum(4)
            multiply_1(4)
            quantise_t(0, 0)
            group_p(0)
            scale_sum(4)
            quantise_t(0, 1)
            finish_1(4)
            transpose(1, 0, 1)
            transpose(1, 1, 0)
            copy_t(1, 0, 0)
            transpose(1, 1, 1)
            row_sum(5)
            copy_t(1, 0, 1)
            scale_sum(5)
            double_1(4)
            store_1(4)

            copy_t(1, 1, 0)
            copy_t(1, 1, 1)
            multiply_1(5)
            sum_on_tensor(6)
            copy_sum(6)
            sum_on_vector(7, 1)
            sum_on_vector(7, 2)
            finish_1(5)
            quantise_p(0)
            double_1(5)
            store_1(5)

            multiply_1(6)
            transpose(2, 0, 0)
            transpose(2, 0, 1)
            row_sum(6)
            scale_sum(6)
            sum_on_vector(7, 3)
            scale_sum(7)
            finish_1(6)
            quantise_t(1, 0)
            group_p(1)
            double_1(6)
            store_1(6)

            multiply_1(7)
            finish_1(7)
            row_sum(7)
            copy_t(2, 0, 0)
            copy_t(2, 0, 1)
            transpose(2, 1, 0)
            quantise_t(1, 1)
            quantise_p(1)
            quantise_t(2, 0)
            double_1(7)
            store_1(7)

            transpose(2, 1, 1)
            copy_t(2, 1, 0)
            copy_t(2, 1, 1)
            for half in range(2):
                transpose(3, 0, half)
                copy_t(3, 0, half)
            transpose(3, 1, 0)
            row_sum(8)
            copy_t(3, 1, 0)
            for i in range(4 * B_PASSES):
                multiply_0(i)
                finish_0(i)
                if i < 3:
                    row_sum(9 + i)
                if i == 4:
                    quantise_t(2, 1)
                if i == 6:
                    quantise_t(3, 0)
                if i == 7:
                    transpose(3, 1, 1)
                    copy_t(3, 1, 1)
                if 8 <= i < 12:
                    row_sum(4 + i)
                if i == 9:
                    quantise_t(3, 1)
